import numpy as np
import ml_dtypes


def mxq(x, axis, fmt="e4m3"):
    dtype, down = {"e4m3": (ml_dtypes.float8_e4m3fn, 7), "e5m2": (ml_dtypes.float8_e5m2, 14)}[fmt]
    v = np.moveaxis(np.asarray(x, np.float32).astype(ml_dtypes.bfloat16).astype(np.float64), axis, -1)
    blocks = v.reshape(v.shape[:-1] + (-1, 32))
    amax = np.abs(blocks).max(-1, keepdims=True)
    byte = np.maximum(np.where(amax > 0, np.frexp(amax)[1] - 1 + 127, 0) - down, 1)
    scale = np.exp2(byte - 127.0)
    codes = (blocks / scale).astype(np.float32).astype(dtype).astype(np.float64)
    return np.moveaxis((codes * scale).reshape(v.shape), -1, axis)


WIDE = False


def mx_kscale(k):
    if not WIDE:
        return np.ones(k)
    levels = np.array([18, -18])
    if k % 512:
        return np.exp2(np.random.permutation(np.resize(levels, k // 32))).repeat(32)
    a = np.empty((k // 512, 16))
    for p in range(k // 512):
        a[p, :8] = np.random.permutation(np.resize(levels, 8))
        for g in range(8):
            far = levels[np.abs(levels - a[p, g]) >= 10]
            a[p, g + 8] = far[np.random.randint(len(far))]
    return np.exp2(a.ravel()).repeat(32)


BF16 = ml_dtypes.bfloat16


def bf(x):
    return np.asarray(x, np.float32).astype(BF16)


def f64(x):
    return np.asarray(x).astype(np.float64)


B, T, D = 512, 4, 1024
EPS = 1e-5


def sigmoid(v):
    e = np.exp(-np.abs(v))
    return np.where(v >= 0.0, 1.0, e) / (1.0 + e)


def silu(v):
    return v * sigmoid(v)


def silu_grad(v):
    sg = sigmoid(v)
    return sg * (1.0 + v * (1.0 - sg))


def setup_inputs():
    r = np.random.standard_normal
    s = mx_kscale(B)
    su = s / s.min()
    u = mx_kscale(D)
    v = mx_kscale(2 * D)
    v1, v2 = v[:D], v[D:]
    x = bf(r((B, T, D)))
    y = bf(r((B, T, D)) * 0.25)
    emb0_0 = bf(r((B, D)))
    We_0 = bf(r((D, 2 * D)) / np.sqrt(D))
    be = bf(r(2 * D) * 0.1)
    g_0 = bf(1.0 + 0.1 * r(D))
    b_0 = bf(r(D) * 0.1)
    Wo_0 = bf(r((D, D)) / np.sqrt(D))
    bo = bf(r(D) * 0.1)
    grad_out = bf(r((B, T, D)) * np.exp2(np.random.randint(-6, 1, (B, T, 1))) / su[:, None, None] * u)
    yf = f64(y)
    mean = yf.mean(-1)
    rstd = 1.0 / np.sqrt(((yf - mean[:, :, None]) ** 2).mean(-1) + EPS)
    n = (yf - mean[:, :, None]) * rstd[:, :, None] * f64(g_0) + f64(b_0)
    e = silu(f64(emb0_0)) @ f64(We_0) + f64(be)
    h = n * (1.0 + e[:, None, :D]) + e[:, None, D:]
    return {
        "x": x,
        "y": y,
        "emb0": bf(f64(emb0_0) * su[:, None]),
        "We": bf(f64(We_0) / v),
        "be": be,
        "ln2_g": bf(f64(g_0) * (v1 / v2)),
        "ln2_b": bf(f64(b_0) * (v1 / v2)),
        "Wo": bf(f64(Wo_0) * v2[:, None] / u),
        "bo": bo,
        "h": np.asarray(h, np.float32),
        "mean": np.asarray(mean, np.float32),
        "rstd": np.asarray(rstd, np.float32),
        "grad_out": grad_out,
    }


def reference(x, y, emb0, We, be, ln2_g, ln2_b, Wo, bo, h, mean, rstd, grad_out):
    g2 = f64(grad_out).reshape(B * T, D)
    da = mxq(g2, 1, "e5m2") @ mxq(f64(Wo), 1, "e4m3").T
    dh = da.reshape(B, T, D) * silu_grad(f64(h))
    n = (f64(y) - f64(mean)[:, :, None]) * f64(rstd)[:, :, None] * f64(ln2_g) + f64(ln2_b)
    de = np.concatenate([(dh * n).sum(1), dh.sum(1)], axis=1)
    ef = f64(emb0)
    ds = mxq(de, 1, "e5m2") @ mxq(f64(We), 1, "e4m3").T
    demb0 = ds * silu_grad(ef)
    dWe = mxq(silu(ef), 0, "e4m3").T @ mxq(de, 0, "e5m2")
    return demb0, dWe

@@ -1,0 +1,633 @@
+from contextlib import ExitStack
+
+import concourse.mybir as mybir
+from concourse.masks import make_identity
+
+B, T, D = 512, 4, 1024
+FLOPS = 2 * B * T * D * D + 2 * (2 * B * 2 * D * D)
+BYTES = 2 * B * T * D * 2 + B * T * D * 4 + B * D * 2 + 3 * D * D * 2 + 2 * D * 2 + 2 * B * T * 4 + B * D * 4 + 2 * D * D * 4
+
+F32 = mybir.dt.float32
+BF16 = mybir.dt.bfloat16
+U32 = mybir.dt.uint32
+U8 = mybir.dt.uint8
+E4 = mybir.dt.float8_e4m3fn_x4
+E5 = mybir.dt.float8_e5m2_x4
+ACT = mybir.ActivationFunctionType
+ALU = mybir.AluOpType
+
+P = 128
+N = 512
+SCALE, SHIFT = 0, 1
+NORM_ACT = ((2, 3), (2, 3), (), (3,), (3,), (), ())
+ON_DVE = ((1, 5), (0, 5))
+WARM = 5
+RAW = 3
+ET = 1
+KEEP = 1
+
+
+def tile_temporalcrossattention_pa_v_kernel(
+    tc, x, y, emb0, We, be, ln2_g, ln2_b, Wo, bo, h, mean, rstd, grad_out, out_0, out_1
+):
+    nc = tc.nc
+    with ExitStack() as ctx:
+        keep = ctx.enter_context(tc.tile_pool(name="keep", bufs=1))
+        work = ctx.enter_context(tc.tile_pool(name="work", bufs=1))
+        psum = ctx.enter_context(tc.psum_pool(name="psum", bufs=1))
+        ctx.enter_context(tc.manual_schedule())
+
+        def mx_pair(name, width):
+            codes = keep.tile([P, width], U32, name=name + "_codes", align_bytes=64)
+            scales = keep.tile([P, width], U8, name=name + "_scales", align_bytes=64)
+            return codes, scales
+
+        g_mx = mx_pair("grad", 4096)
+        wo_mx = mx_pair("wo", 2048)
+        we_mx = mx_pair("we", 4096)
+        e_mx = mx_pair("emb", 1024)
+        df_mx = mx_pair("de_f", 2048)
+        db_mx = mx_pair("de_b", 1024)
+
+        ident = keep.tile([P, P], F32)
+        make_identity(nc, ident[:])
+        mean_sb = keep.tile([P, 2, 8], F32)
+        rstd_sb = keep.tile([P, 2, 8], F32)
+        gb_raw = keep.tile([P, 2, 16], BF16)
+        gb = keep.tile([P, 2, 8], F32)
+        shift_sb = keep.tile([P, 2, 8], F32)
+        warm = keep.tile([P, N], BF16)
+
+        raws, grps, hs, ys, sil, tnh, prod, das, sums, xs, des, gis, ers, eas, stages, dhs, ets = (
+            {}, {}, {}, {}, {}, {}, {}, {}, {}, {}, {}, {}, {}, {}, {}, {}, {})
+
+        def seqs(c):
+            u, hi = divmod(c, 2)
+            return slice(256 * hi + u, 256 * (hi + 1), 2)
+
+        def cols(half):
+            return slice(N * half, N * (half + 1))
+
+        def raw_tile(key):
+            raws[key] = work.tile([P, 4096], BF16, name="raw", tag="raw", bufs=RAW, align_bytes=64)
+            return raws[key]
+
+        def load_grad(c, pair):
+            key = ("g", c)
+            raw = raws[key] if key in raws else raw_tile(key)
+            nc.sync.dma_start(
+                out=raw[:, 2048 * pair : 2048 * (pair + 1)],
+                in_=grad_out[seqs(c), 2 * pair : 2 * pair + 2, :].rearrange("q t k -> q (t k)"),
+            )
+
+        def load_wo(half, pair):
+            key = ("wo", half)
+            raw = raws[key] if key in raws else raw_tile(key)
+            rows = Wo[cols(half), :].rearrange("(m t) k -> m (t k)", t=4)
+            nc.sync.dma_start(out=raw[:, 2048 * pair : 2048 * (pair + 1)], in_=rows[:, 2048 * pair : 2048 * (pair + 1)])
+
+        def load_we(n, part):
+            raw = raw_tile(("we", n, part))
+            nc.sync.dma_start(
+                out=raw[:].rearrange("p (a f) -> p a f", a=4),
+                in_=We[cols(n), D * part : D * (part + 1)].rearrange("(a p) f -> p a f", p=P),
+            )
+
+        def load_emb():
+            raw = raw_tile("emb")
+            nc.sync.dma_start(out=raw[:], in_=emb0.rearrange("(p j) d -> p (j d)", j=4))
+
+        def load_emb_rows(c):
+            ers[c] = work.tile([P, D], BF16, name="er", tag="er", bufs=2)
+            nc.sync.dma_start(out=ers[c][:], in_=emb0[seqs(c), :])
+
+        def load_h(k, pair):
+            half, c = divmod(k, 4)
+            hs[k, pair] = work.tile([P, 2, N], F32, name="hh", tag="hh", bufs=4)
+            nc.sync.dma_start(out=hs[k, pair][:], in_=h[seqs(c), 2 * pair : 2 * pair + 2, cols(half)])
+
+        def load_y(k):
+            half, c = divmod(k, 4)
+            ys[k] = work.tile([P, T, N], BF16, name="yy", tag="yy", bufs=3)
+            nc.sync.dma_start(out=ys[k][:], in_=y[seqs(c), :, cols(half)])
+
+        def load_stats():
+            nc.sync.dma_start(out=mean_sb[:], in_=mean.rearrange("(hi q u) t -> q hi (u t)", hi=2, u=2))
+            nc.sync.dma_start(out=rstd_sb[:], in_=rstd.rearrange("(hi q u) t -> q hi (u t)", hi=2, u=2))
+
+        def load_gain_bias():
+            for i, vec in enumerate((ln2_g, ln2_b)):
+                nc.sync.dma_start(
+                    out=gb_raw[:, i, 0:8].rearrange("p (a t) -> p a t", a=2),
+                    in_=vec.rearrange("(a p t) -> p a t", a=2, t=4),
+                )
+
+        def bank(tag):
+            depth = {"da": 3, "s0": 1, "s1": 1, "misc": 3}[tag]
+            return psum.tile([P, N], F32, name=tag, tag=tag, bufs=depth)
+
+        def copy_on(eng, out, in_):
+            if eng == "act":
+                nc.scalar.copy(out=out, in_=in_)
+            else:
+                nc.vector.tensor_copy(out=out, in_=in_)
+
+        def grp_tile(key):
+            if key not in grps:
+                grps[key] = work.tile([P, 2048], BF16, name="grp", tag="grp", bufs=4, align_bytes=64)
+            return grps[key]
+
+        def turn(sources, tag="misc"):
+            ps = bank(tag)
+            for i, src in enumerate(sources):
+                nc.tensor.transpose(ps[:, P * i : P * (i + 1)], src, ident[:])
+            return ps
+
+        def gather(eng, ps, key, slot):
+            words = grp_tile(key)[:].bitcast(F32)[:, N * slot : N * (slot + 1)]
+            copy_on(eng, words.rearrange("p (a m u) -> p a m u", a=2, u=2), ps[:].rearrange("p (a u m) -> p a m u", a=2, u=2))
+
+        def every_2nd(key, first):
+            words = raws[key][:].bitcast(F32)
+            return [words[:, w + u : w + 256 : 2] for w in first for u in (0, 1)]
+
+        def turn_grad(c, f):
+            return turn(every_2nd(("g", c), (512 * f, 512 * f + 256))), ("g", c, f // 2), f % 2
+
+        def turn_wo(half, g, pair):
+            return turn(every_2nd(("wo", half), (1024 * pair + 256 * g, 1024 * pair + 512 + 256 * g))), ("wo", half, g), pair
+
+        def turn_we(n, part, half, pair):
+            first = (1024 * pair + 256 * half, 1024 * pair + 512 + 256 * half)
+            return turn(every_2nd(("we", n, part), first)), ("we", n, part, half), pair
+
+        def turn_de(half, part, pair, tag="misc"):
+            words = des[half][:].rearrange("p a t b -> p (a t b)").bitcast(F32)
+            first = [(4 * part + 2 * pair + a) * 256 + P * u for a in (0, 1) for u in (0, 1)]
+            return turn([words[:, w : w + P] for w in first], tag), ("de", half, part), pair
+
+        def quant(src, mx, first, width, fmt):
+            nc.vector.quantize_mx(
+                out=mx[0][:, first : first + width].bitcast(fmt), scales=mx[1][:, first : first + width], in_=src
+            )
+
+        def quant_grad(c, pair):
+            quant(grps["g", c, pair][:], g_mx, 1024 * c + N * pair, N, E5)
+
+        def quant_wo(half, g):
+            quant(grps["wo", half, g][:], wo_mx, 1024 * half + N * g, N, E4)
+
+        def quant_we(n, part, half):
+            quant(grps["we", n, part, half][:], we_mx, 2048 * part + 1024 * half + N * n, N, E4)
+
+        def quant_de_b(half, part):
+            quant(grps["de", half, part][:], db_mx, N * part, N, E5)
+
+        def mx(ps, lhs, l0, lfmt, rhs, r0, rfmt, start, stop):
+            nc.tensor.matmul_mx(
+                out=ps[:],
+                lhsT=lhs[0][:, l0 : l0 + P].bitcast(lfmt),
+                lhsT_scale=lhs[1][:, l0 : l0 + P],
+                rhs=rhs[0][:, r0 : r0 + N].bitcast(rfmt),
+                rhs_scale=rhs[1][:, r0 : r0 + N],
+                start=start,
+                stop=stop,
+            )
+
+        def mm(k, f):
+            half, c = divmod(k, 4)
+            das[k, f] = bank("da")
+            for g in (0, 1):
+                mx(das[k, f], g_mx, 1024 * c + 256 * f + P * g, E5, wo_mx, 1024 * half + N * g, E4, g == 0, g == 1)
+
+        def sorted_h(k, pair):
+            return hs[k, pair][:].rearrange("p f (j e) -> p f e j", e=2)
+
+        def silu_h(k, pair):
+            sil[k, pair] = work.tile([P, 2 * N], F32, name="sil", tag="sil", bufs=3)
+            out = sil[k, pair][:].rearrange("p (f e j) -> p f e j", f=2, e=2)
+            nc.scalar.activation(out=out, in_=sorted_h(k, pair), func=ACT.Silu, scale=-1.0)
+
+        def tanh_h(k, pair):
+            tnh[k, pair] = work.tile([P, 2 * N], F32, name="tnh", tag="tnh", bufs=3)
+            out = tnh[k, pair][:].rearrange("p (f e j) -> p f e j", f=2, e=2)
+            nc.scalar.activation(out=out, in_=sorted_h(k, pair), func=ACT.Tanh, scale=0.5)
+
+        def gate_da(k, f):
+            if f % 2 == 0:
+                dhs[k, f // 2] = work.tile([P, 2, 2, 256], F32, name="dh", tag="dh", bufs=3)
+            nc.vector.scalar_tensor_tensor(
+                out=dhs[k, f // 2][:, :, f % 2, :],
+                in0=tnh[k, f // 2][:, cols(f % 2)].rearrange("p (r v) -> p v r", v=2),
+                scalar=1.0,
+                in1=das[k, f][:].rearrange("p (v r) -> p v r", v=2),
+                op0=ALU.add,
+                op1=ALU.mult,
+            )
+
+        def norm_y(k, f, eng="dve"):
+            c = k % 4
+            u, hi = divmod(c, 2)
+            if (k, f // 2) not in prod:
+                prod[k, f // 2] = work.tile([P, 2, 2, 256], F32, name="prod", tag="prod", bufs=3)
+            j = 4 * u + f
+            if eng == "act":
+                nc.scalar.activation(
+                    out=prod[k, f // 2][:, :, f % 2, :].rearrange("p v (e m) -> p v e m", e=2),
+                    in_=ys[k][:, f, :].rearrange("p (m v e) -> p v e m", v=2, e=2),
+                    func=ACT.Identity,
+                    scale=rstd_sb[:, hi, j : j + 1],
+                    bias=shift_sb[:, hi, j : j + 1],
+                )
+                return
+            nc.vector.tensor_scalar(
+                out=prod[k, f // 2][:, :, f % 2, :].rearrange("p v (e m) -> p v e m", e=2),
+                in0=ys[k][:, f, :].rearrange("p (m v e) -> p v e m", v=2, e=2),
+                scalar1=mean_sb[:, hi, j : j + 1],
+                scalar2=rstd_sb[:, hi, j : j + 1],
+                op0=ALU.subtract,
+                op1=ALU.mult,
+            )
+
+        def make_dh(k, pair):
+            dh = dhs[k, pair][:].rearrange("p v f r -> p v (f r)")
+            a = sil[k, pair][:].rearrange("p (r v) -> p v r", v=2)
+            nc.vector.scalar_tensor_tensor(out=dh, in0=a, scalar=1.0, in1=dh, op0=ALU.subtract, op1=ALU.mult)
+
+        def make_prod(k, pair):
+            p = prod[k, pair][:]
+            nc.vector.tensor_tensor(out=p, in0=p, in1=dhs[k, pair][:], op=ALU.mult)
+
+        def sum_frames(k, part):
+            src = prod if part == SCALE else dhs
+            ps = bank("s1" if part == SCALE else "s0")
+            sums[k, part] = ps
+            for t in range(4):
+                for f in range(T):
+                    block = src[k, f // 2][:, t // 2, f % 2, P * (t % 2) : P * (t % 2 + 1)]
+                    nc.tensor.matmul(
+                        ps[:, P * t : P * (t + 1)], lhsT=block, rhs=ident[:],
+                        start=(f == 0), stop=(f == T - 1), is_transpose=True,
+                    )
+
+        def de_tile(half):
+            if half not in des:
+                des[half] = work.tile([P, 2, 4, B], BF16, name="de", tag="de", bufs=2, align_bytes=64)
+            return des[half]
+
+        def de_shift(k):
+            half, c = divmod(k, 4)
+            nc.scalar.activation(
+                out=de_tile(half)[:, SHIFT, :, P * c : P * (c + 1)],
+                in_=sums[k, SHIFT][:].rearrange("p (t q) -> p t q", t=4), func=ACT.Copy, scale=0.25,
+            )
+
+        def gain_term(k):
+            half = k // 4
+            xs[k] = work.tile([P, N], F32, name="xs", tag="xs", bufs=1)
+            for t in range(4):
+                nc.scalar.activation(
+                    out=xs[k][:, P * t : P * (t + 1)], in_=sums[k, SCALE][:, P * t : P * (t + 1)],
+                    func=ACT.Copy, scale=gb[:, 0, 4 * half + t : 4 * half + t + 1],
+                )
+
+        def de_scale(k):
+            half, c = divmod(k, 4)
+            for t in range(4):
+                nc.vector.scalar_tensor_tensor(
+                    out=de_tile(half)[:, SCALE, t, P * c : P * (c + 1)],
+                    in0=sums[k, SHIFT][:, P * t : P * (t + 1)],
+                    scalar=gb[:, 1, 4 * half + t : 4 * half + t + 1],
+                    in1=xs[k][:, P * t : P * (t + 1)], op0=ALU.mult, op1=ALU.add,
+                )
+
+        def weave_de(k):
+            half, c = divmod(k, 4)
+            gis[k] = work.tile([P, 2, P, 4], BF16, name="gi", tag="gi", bufs=2, align_bytes=64)
+            nc.vector.tensor_copy(out=gis[k][:], in_=des[half][:, :, :, P * c : P * (c + 1)].rearrange("p a t q -> p a q t"))
+
+        def quant_de_f(k):
+            quant(gis[k][:].rearrange("p a q t -> p (a q t)"), df_mx, 256 * k, 256, E5)
+
+        def silu_emb(n):
+            src = raws["emb"][:].rearrange("p (e u d) -> p d u e", e=2, u=2)[:, cols(n), :, :]
+            out = grp_tile(("e", n))[:].rearrange("p (d u e) -> p d u e", u=2, e=2)
+            nc.scalar.activation(out=out, in_=src, func=ACT.Silu)
+
+        def quant_emb(n):
+            quant(grps["e", n][:], e_mx, N * n, N, E4)
+
+        def emb_tanh(c):
+            tag, depth = ("et", ET) if c < 2 else ("tnh", 3)
+            ets[c] = work.tile([P, D], F32, name=tag, tag=tag, bufs=depth)
+            nc.scalar.activation(out=ets[c][:], in_=ers[c][:], func=ACT.Tanh, scale=0.5)
+
+        def emb_silu(c):
+            tag, depth = ("ea", 2) if c < 2 else ("sil", 3)
+            eas[c] = work.tile([P, D], F32, name=tag, tag=tag, bufs=depth)
+            nc.scalar.activation(out=eas[c][:], in_=ers[c][:], func=ACT.Silu, scale=-1.0)
+
+        def emb_acts(c):
+            emb_tanh(c)
+            emb_silu(c)
+
+        def out0_mm(c, n, tag="misc"):
+            ps = bank(tag)
+            passes = [(half, part) for half in (0, 1) for part in (SHIFT, SCALE)]
+            for i, (half, part) in enumerate(passes):
+                mx(ps, df_mx, 256 * (4 * half + c) + P * part, E5, we_mx, 2048 * part + 1024 * half + N * n, E4, i == 0, i == 3)
+            return ps
+
+        def out0_gate(c, n, ps):
+            part = ets[c][:, cols(n)]
+            nc.vector.scalar_tensor_tensor(out=part, in0=part, scalar=1.0, in1=ps[:], op0=ALU.add, op1=ALU.mult)
+
+        def out0_end(c):
+            ea, et = eas[c], ets[c]
+            nc.vector.scalar_tensor_tensor(out=ea[:], in0=ea[:], scalar=1.0, in1=et[:], op0=ALU.subtract, op1=ALU.mult)
+            nc.sync.dma_start(out=out_0[seqs(c), :], in_=ea[:])
+
+        def out1_mm(part, m, tag="misc"):
+            ps = bank(tag)
+            mx(ps, e_mx, P * m, E4, db_mx, N * part, E5, True, True)
+            return ps
+
+        def out1_copy(eng, half, part, m, ps):
+            key = (half, part, m // 2)
+            if key not in stages:
+                if half == 1 and m % 4 < 2:
+                    stages[key] = work.tile([P, 2, N], F32, name="hh", tag="hh", bufs=4)
+                else:
+                    stages[key] = work.tile([P, 2, N], F32, name="stage", tag="stage", bufs=3)
+            out = stages[key][:, m % 2, :].rearrange("p (r t) -> p r t", t=4)
+            src = ps[:].rearrange("p (t r) -> p r t", t=4)
+            if eng == "act":
+                nc.scalar.activation(out=out, in_=src, func=ACT.Copy, scale=-2.0)
+            else:
+                nc.vector.tensor_scalar(out=out, in0=src, scalar1=-2.0, scalar2=None, op0=ALU.mult)
+            if m % 2 == 1:
+                f0 = D * part + N * half
+                rows = out_1[P * (m - 1) : P * (m + 1), f0 : f0 + N].rearrange("(a p) f -> p a f", p=P)
+                nc.sync.dma_start(out=rows, in_=stages[key][:])
+
+        def job(kind, *a):
+            if kind == "out1":
+                ps = out1_mm(a[1], a[2])
+                eng = "dve" if (a[1], a[2]) in ON_DVE else "act"
+                return lambda: out1_copy(eng, a[0], a[1], a[2], ps)
+            turned = {"g": turn_grad, "wo": turn_wo, "we": turn_we, "de": turn_de}[kind](*a)
+            return lambda: gather("act", *turned)
+
+        def run_jobs(jobs):
+            return [job(*j) for j in jobs]
+
+        def finish(copies):
+            for cp in copies:
+                cp()
+
+        we_jobs = [("we", n, part, half, pair) for n in (0, 1) for part in (0, 1) for half in (0, 1) for pair in (0, 1)]
+        o1_jobs = [("out1", 0, part, m) for part in (SHIFT, SCALE) for m in range(8)]
+        de_jobs = [("de", 0, part, pair) for part in (SHIFT, SCALE) for pair in (0, 1)]
+        g_jobs = [("g", c, f) for c in (1, 2, 3) for f in range(T)]
+        wo_jobs = [("wo", 1, g, pair) for g in (0, 1) for pair in (0, 1)]
+        batches = {
+            0: (g_jobs[0:2], g_jobs[2:4], g_jobs[4:6]),
+            1: (g_jobs[6:8], g_jobs[8:10], g_jobs[10:12]),
+            2: (wo_jobs[0:2], wo_jobs[2:4], we_jobs[0:2]),
+            3: (we_jobs[2:5], we_jobs[5:7], we_jobs[7:9]),
+            4: (we_jobs[9:12], we_jobs[12:15], we_jobs[15:16] + de_jobs[0:2]),
+            5: (de_jobs[2:4], o1_jobs[0:3], o1_jobs[3:6]),
+            6: (o1_jobs[6:9], o1_jobs[9:11], o1_jobs[11:14]),
+            7: (o1_jobs[14:16], [], []),
+        }
+
+        def quant_done(jobs):
+            for j in jobs:
+                if j[0] == "g" and j[2] % 2 == 1:
+                    quant_grad(j[1], j[2] // 2)
+                if j[0] == "wo" and j[3] == 1:
+                    quant_wo(j[1], j[2])
+                if j[0] == "we" and j[4] == 1:
+                    quant_we(j[1], j[2], j[3])
+                if j[0] == "de" and j[3] == 1:
+                    quant_de_b(j[1], j[2])
+
+        early_loads = {
+            2: [lambda: load_emb()],
+            4: [lambda: load_we(1, 1)],
+        }
+        extra_loads = {
+            1: [lambda: load_wo(1, 0), lambda: load_wo(1, 1)],
+            3: [lambda: load_we(1, 0)],
+            4: [lambda: load_emb_rows(0), lambda: load_emb_rows(1)],
+        }
+        late_loads = {
+            0: [lambda: load_grad(3, 0), lambda: load_grad(3, 1)],
+            1: [lambda: load_we(0, 0)],
+            2: [lambda: load_we(0, 1)],
+        }
+
+        load_wo(0, 0)
+        load_grad(0, 0)
+        load_wo(0, 1)
+        load_h(0, 0)
+        load_grad(0, 1)
+        load_stats()
+        load_y(0)
+        load_h(0, 1)
+        load_grad(1, 0)
+        load_h(1, 0)
+        load_gain_bias()
+        load_grad(1, 1)
+        load_y(1)
+        load_h(1, 1)
+
+        nc.vector.memset(warm[:], 0.0)
+        spare = bank("s1")
+
+        def keep_clock(count):
+            for i in range(count):
+                nc.tensor.matmul(spare[:], lhsT=warm[:, 0:P], rhs=warm[:], start=True, stop=True)
+
+        keep_clock(WARM)
+        gather("dve", *turn_wo(0, 0, 0))
+        gather("act", *turn_wo(0, 1, 0))
+        keep_clock(KEEP)
+        gather("dve", *turn_grad(0, 0))
+        gather("act", *turn_grad(0, 1))
+        keep_clock(KEEP)
+        gather("dve", *turn_wo(0, 0, 1))
+        quant_grad(0, 0)
+        gather("dve", *turn_wo(0, 1, 1))
+        tanh_h(0, 0)
+        silu_h(0, 0)
+        quant_wo(0, 0)
+        quant_wo(0, 1)
+        t0 = turn_grad(0, 2)
+        t1 = turn_grad(0, 3)
+        load_grad(2, 0)
+        load_grad(2, 1)
+        mm(0, 0)
+        mm(0, 1)
+        gather("act", *t0)
+        gather("act", *t1)
+        copies = run_jobs(batches[0][0])
+        nc.vector.scalar_tensor_tensor(
+            out=shift_sb[:], in0=mean_sb[:], scalar=-1.0, in1=rstd_sb[:], op0=ALU.mult, op1=ALU.mult
+        )
+        tanh_h(0, 1)
+        silu_h(0, 1)
+
+        pending = []
+        for k in range(7):
+            first = k == 0
+            b1, b2, b3 = batches[k]
+            on_act = NORM_ACT[k]
+            for ld in early_loads.get(k, []):
+                ld()
+            if k + 2 < 8:
+                load_h(k + 2, 0)
+                load_y(k + 2)
+            gate_da(k, 0)
+            if not first:
+                sum_frames(k - 1, SCALE)
+            norm_y(k, 0)
+            gate_da(k, 1)
+            if first:
+                quant_grad(0, 1)
+                mm(0, 2)
+            norm_y(k, 1)
+            mm(k, 3)
+            silu_h(k + 1, 0)
+            if not first:
+                de_shift(k - 1)
+                gain_term(k - 1)
+            if not first:
+                copies = run_jobs(b1)
+            tanh_h(k + 1, 0)
+            finish(copies)
+            for f in on_act:
+                norm_y(k, f, "act")
+            if k + 2 < 8:
+                load_h(k + 2, 1)
+            make_dh(k, 0)
+            quant_done(pending)
+            if first:
+                nc.vector.tensor_scalar(out=gb[:], in0=gb_raw[:, :, 0:8], scalar1=0.25, scalar2=None, op0=ALU.mult)
+            if k == 3:
+                quant_emb(0)
+            if k == 4:
+                quant_emb(1)
+            for ld in extra_loads.get(k, []):
+                ld()
+            if not first:
+                de_scale(k - 1)
+            make_prod(k, 0)
+            if not first:
+                weave_de(k - 1)
+            outs = [out0_mm(0, n, ("s1", "s0")[n]) for n in (0, 1)] if k == 6 else []
+            gate_da(k, 2)
+            quant_done(b1)
+            mm(k + 1, 0)
+            copies = run_jobs(b2)
+            silu_h(k + 1, 1)
+            finish(copies)
+            for ld in late_loads.get(k, []):
+                ld()
+            if 2 not in on_act:
+                norm_y(k, 2)
+            gate_da(k, 3)
+            if not first:
+                quant_de_f(k - 1)
+            if 3 not in on_act:
+                norm_y(k, 3)
+            for n, ps in enumerate(outs):
+                out0_gate(0, n, ps)
+            mm(k + 1, 1)
+            copies = run_jobs(b3)
+            tanh_h(k + 1, 1)
+            finish(copies)
+            if k in (2, 3):
+                silu_emb(k - 2)
+            if k == 5:
+                emb_acts(0)
+            make_dh(k, 1)
+            quant_done(b2)
+            if outs:
+                out0_end(0)
+                load_emb_rows(2)
+            mm(k + 1, 2)
+            sum_frames(k, SHIFT)
+            make_prod(k, 1)
+            if k == 6:
+                emb_acts(1)
+            pending = b3
+
+        load_emb_rows(3)
+        gate_da(7, 0)
+        sum_frames(6, SCALE)
+        gate_da(7, 1)
+        mm(7, 3)
+        norm_y(7, 0, "act")
+        de_shift(6)
+        gain_term(6)
+        norm_y(7, 1, "act")
+        gate_da(7, 2)
+        make_dh(7, 0)
+        gate_da(7, 3)
+        de_scale(6)
+        make_dh(7, 1)
+        outs = [out0_mm(1, n, "da") for n in (0, 1)]
+        norm_y(7, 2, "act")
+        norm_y(7, 3, "act")
+        sum_frames(7, SHIFT)
+        emb_tanh(2)
+        make_prod(7, 0)
+        make_prod(7, 1)
+        de_shift(7)
+        copies = run_jobs(batches[7][0])
+        t0 = turn_de(1, SHIFT, 0, "misc")
+        t1 = turn_de(1, SHIFT, 1, "da")
+        sum_frames(7, SCALE)
+        finish(copies)
+        for n, ps in enumerate(outs):
+            out0_gate(1, n, ps)
+        gather("act", *t0)
+        gather("dve", *t1)
+        emb_silu(2)
+        weave_de(6)
+        quant_de_b(1, SHIFT)
+        gain_term(7)
+        out0_end(1)
+        de_scale(7)
+        quant_de_f(6)
+        tags = ("misc", "da")
+        for m in range(4):
+            out1_copy("act", 1, SHIFT, m, out1_mm(SHIFT, m, tags[m % 2]))
+        t0 = turn_de(1, SCALE, 0, "s0")
+        t1 = turn_de(1, SCALE, 1, "s1")
+        gather("dve", *t0)
+        gather("dve", *t1)
+        for m in range(4, 8):
+            out1_copy("act", 1, SHIFT, m, out1_mm(SHIFT, m, tags[m % 2]))
+        weave_de(7)
+        quant_de_b(1, SCALE)
+        outs = [out0_mm(2, n, ("s0", "s1")[n]) for n in (0, 1)]
+        quant_de_f(7)
+        for n, ps in enumerate(outs):
+            out0_gate(2, n, ps)
+        emb_tanh(3)
+        for m in range(0, 2):
+            out1_copy("dve", 1, SCALE, m, out1_mm(SCALE, m, tags[m % 2]))
+        for m in range(2, 4):
+            out1_copy("act", 1, SCALE, m, out1_mm(SCALE, m, tags[m % 2]))
+        out0_end(2)
+        outs = [out0_mm(3, n, ("s0", "s1")[n]) for n in (0, 1)]
+        emb_silu(3)
+        for n, ps in enumerate(outs):
+            out0_gate(3, n, ps)
+        for m in range(4, 6):
+            out1_copy("act", 1, SCALE, m, out1_mm(SCALE, m, tags[m % 2]))
+        out0_end(3)
+        out1_copy("act", 1, SCALE, 6, out1_mm(SCALE, 6, "misc"))
+        out1_copy("dve", 1, SCALE, 7, out1_mm(SCALE, 7, "da"))

@@ -19,9 +19,11 @@ ALU = mybir.AluOpType
 P = 128
 N = 512
 SCALE, SHIFT = 0, 1
-NORM_ACT = ((2, 3), (2, 3), (), (3,), (3,), (), ())
-ON_DVE = ((1, 5), (0, 5))
+NORM_ACT = ((), (), (), (), (), (), ())
+ON_DVE = (("g", 1, 0), ("g", 1, 1))
 WARM = 5
+LAST = "pool"
+FILL = 0
 RAW = 3
 ET = 1
 KEEP = 1
@@ -55,11 +57,10 @@ def tile_temporalcrossattention_pa_v_kernel(
         rstd_sb = keep.tile([P, 2, 8], F32)
         gb_raw = keep.tile([P, 2, 16], BF16)
         gb = keep.tile([P, 2, 8], F32)
-        shift_sb = keep.tile([P, 2, 8], F32)
         warm = keep.tile([P, N], BF16)
 
-        raws, grps, hs, ys, sil, tnh, prod, das, sums, xs, des, gis, ers, eas, stages, dhs, ets = (
-            {}, {}, {}, {}, {}, {}, {}, {}, {}, {}, {}, {}, {}, {}, {}, {}, {})
+        raws, grps, hs, ys, sil, tnh, prod, das, sums, xs, des, gis, ers, eas, stages, dhs, ets, negs = (
+            {}, {}, {}, {}, {}, {}, {}, {}, {}, {}, {}, {}, {}, {}, {}, {}, {}, {})
 
         def seqs(c):
             u, hi = divmod(c, 2)
@@ -108,7 +109,7 @@ def tile_temporalcrossattention_pa_v_kernel(
 
         def load_y(k):
             half, c = divmod(k, 4)
-            ys[k] = work.tile([P, T, N], BF16, name="yy", tag="yy", bufs=3)
+            ys[k] = work.tile([P, T, N], BF16, name="yy", tag="yy", bufs=2)
             nc.sync.dma_start(out=ys[k][:], in_=y[seqs(c), :, cols(half)])
 
         def load_stats():
@@ -215,7 +216,7 @@ def tile_temporalcrossattention_pa_v_kernel(
 
         def gate_da(k, f):
             if f % 2 == 0:
-                dhs[k, f // 2] = work.tile([P, 2, 2, 256], F32, name="dh", tag="dh", bufs=3)
+                dhs[k, f // 2] = work.tile([P, 2, 2, 256], F32, name="dh", tag="dh", bufs=4)
             nc.vector.scalar_tensor_tensor(
                 out=dhs[k, f // 2][:, :, f % 2, :],
                 in0=tnh[k, f // 2][:, cols(f % 2)].rearrange("p (r v) -> p v r", v=2),
@@ -231,13 +232,14 @@ def tile_temporalcrossattention_pa_v_kernel(
             if (k, f // 2) not in prod:
                 prod[k, f // 2] = work.tile([P, 2, 2, 256], F32, name="prod", tag="prod", bufs=3)
             j = 4 * u + f
-            if eng == "act":
-                nc.scalar.activation(
+            if eng == "pool":
+                nc.gpsimd.tensor_scalar(
                     out=prod[k, f // 2][:, :, f % 2, :].rearrange("p v (e m) -> p v e m", e=2),
-                    in_=ys[k][:, f, :].rearrange("p (m v e) -> p v e m", v=2, e=2),
-                    func=ACT.Identity,
-                    scale=rstd_sb[:, hi, j : j + 1],
-                    bias=shift_sb[:, hi, j : j + 1],
+                    in0=ys[k][:, f, :].rearrange("p (m v e) -> p v e m", v=2, e=2),
+                    scalar1=negs[k, f // 2][:, f % 2 : f % 2 + 1],
+                    scalar2=rstd_sb[:, hi, j : j + 1],
+                    op0=ALU.add,
+                    op1=ALU.mult,
                 )
                 return
             nc.vector.tensor_scalar(
@@ -247,6 +249,14 @@ def tile_temporalcrossattention_pa_v_kernel(
                 scalar2=rstd_sb[:, hi, j : j + 1],
                 op0=ALU.subtract,
                 op1=ALU.mult,
+            )
+
+        def negate_mean(k, pair):
+            u, hi = divmod(k % 4, 2)
+            j = 4 * u + 2 * pair
+            negs[k, pair] = work.tile([P, 2], F32, name="neg", tag="neg", bufs=4)
+            nc.vector.tensor_scalar(
+                out=negs[k, pair][:], in0=mean_sb[:, hi, j : j + 2], scalar1=-1.0, scalar2=None, op0=ALU.mult
             )
 
         def make_dh(k, pair):
@@ -318,7 +328,7 @@ def tile_temporalcrossattention_pa_v_kernel(
             quant(grps["e", n][:], e_mx, N * n, N, E4)
 
         def emb_tanh(c):
-            tag, depth = ("et", ET) if c < 2 else ("tnh", 3)
+            tag, depth = ("et", 1) if c == 0 else ("tnh", 3)
             ets[c] = work.tile([P, D], F32, name=tag, tag=tag, bufs=depth)
             nc.scalar.activation(out=ets[c][:], in_=ers[c][:], func=ACT.Tanh, scale=0.5)
 
@@ -373,10 +383,11 @@ def tile_temporalcrossattention_pa_v_kernel(
         def job(kind, *a):
             if kind == "out1":
                 ps = out1_mm(a[1], a[2])
-                eng = "dve" if (a[1], a[2]) in ON_DVE else "act"
+                eng = "dve" if (kind,) + a in ON_DVE else "act"
                 return lambda: out1_copy(eng, a[0], a[1], a[2], ps)
             turned = {"g": turn_grad, "wo": turn_wo, "we": turn_we, "de": turn_de}[kind](*a)
-            return lambda: gather("act", *turned)
+            eng = "dve" if (kind,) + a in ON_DVE else "act"
+            return lambda: gather(eng, *turned)
 
         def run_jobs(jobs):
             return [job(*j) for j in jobs]
@@ -391,11 +402,11 @@ def tile_temporalcrossattention_pa_v_kernel(
         g_jobs = [("g", c, f) for c in (1, 2, 3) for f in range(T)]
         wo_jobs = [("wo", 1, g, pair) for g in (0, 1) for pair in (0, 1)]
         batches = {
-            0: (g_jobs[0:2], g_jobs[2:4], g_jobs[4:6]),
-            1: (g_jobs[6:8], g_jobs[8:10], g_jobs[10:12]),
-            2: (wo_jobs[0:2], wo_jobs[2:4], we_jobs[0:2]),
-            3: (we_jobs[2:5], we_jobs[5:7], we_jobs[7:9]),
-            4: (we_jobs[9:12], we_jobs[12:15], we_jobs[15:16] + de_jobs[0:2]),
+            0: (g_jobs[2:4], g_jobs[4:6], g_jobs[6:8]),
+            1: (g_jobs[8:10], g_jobs[10:12], wo_jobs[0:2]),
+            2: (wo_jobs[2:4], we_jobs[0:2], we_jobs[2:4]),
+            3: (we_jobs[4:6], we_jobs[6:8], we_jobs[8:10]),
+            4: (we_jobs[10:13], we_jobs[13:16], de_jobs[0:2]),
             5: (de_jobs[2:4], o1_jobs[0:3], o1_jobs[3:6]),
             6: (o1_jobs[6:9], o1_jobs[9:11], o1_jobs[11:14]),
             7: (o1_jobs[14:16], [], []),
@@ -413,23 +424,24 @@ def tile_temporalcrossattention_pa_v_kernel(
                     quant_de_b(j[1], j[2])
 
         early_loads = {
-            2: [lambda: load_emb()],
+            0: [lambda: load_grad(3, 0), lambda: load_grad(3, 1)],
+            1: [lambda: load_we(0, 0)],
+            3: [lambda: load_we(1, 0)],
             4: [lambda: load_we(1, 1)],
+            6: [lambda: load_emb_rows(2)],
         }
         extra_loads = {
-            1: [lambda: load_wo(1, 0), lambda: load_wo(1, 1)],
-            3: [lambda: load_we(1, 0)],
+            0: [lambda: load_wo(1, 0), lambda: load_wo(1, 1)],
+            2: [lambda: load_we(0, 1)],
             4: [lambda: load_emb_rows(0), lambda: load_emb_rows(1)],
         }
         late_loads = {
-            0: [lambda: load_grad(3, 0), lambda: load_grad(3, 1)],
-            1: [lambda: load_we(0, 0)],
-            2: [lambda: load_we(0, 1)],
+            1: [lambda: load_emb()],
         }
 
         load_wo(0, 0)
-        load_grad(0, 0)
         load_wo(0, 1)
+        load_grad(0, 0)
         load_h(0, 0)
         load_grad(0, 1)
         load_stats()
@@ -437,15 +449,13 @@ def tile_temporalcrossattention_pa_v_kernel(
         load_h(0, 1)
         load_grad(1, 0)
         load_h(1, 0)
-        load_gain_bias()
         load_grad(1, 1)
-        load_y(1)
         load_h(1, 1)
 
         nc.vector.memset(warm[:], 0.0)
-        spare = bank("s1")
 
         def keep_clock(count):
+            spare = bank("s1")
             for i in range(count):
                 nc.tensor.matmul(spare[:], lhsT=warm[:, 0:P], rhs=warm[:], start=True, stop=True)
 
@@ -453,110 +463,107 @@ def tile_temporalcrossattention_pa_v_kernel(
         gather("dve", *turn_wo(0, 0, 0))
         gather("act", *turn_wo(0, 1, 0))
         keep_clock(KEEP)
-        gather("dve", *turn_grad(0, 0))
-        gather("act", *turn_grad(0, 1))
-        keep_clock(KEEP)
         gather("dve", *turn_wo(0, 0, 1))
-        quant_grad(0, 0)
-        gather("dve", *turn_wo(0, 1, 1))
-        tanh_h(0, 0)
-        silu_h(0, 0)
+        gather("act", *turn_wo(0, 1, 1))
+        keep_clock(KEEP)
+        t0 = turn_grad(0, 0)
+        t1 = turn_grad(0, 1)
         quant_wo(0, 0)
+        gather("act", *t0)
         quant_wo(0, 1)
+        gather("dve", *t1)
+        tanh_h(0, 0)
+        keep_clock(KEEP)
         t0 = turn_grad(0, 2)
         t1 = turn_grad(0, 3)
+        quant_grad(0, 0)
         load_grad(2, 0)
+        load_y(1)
         load_grad(2, 1)
+        load_gain_bias()
         mm(0, 0)
         mm(0, 1)
         gather("act", *t0)
-        gather("act", *t1)
-        copies = run_jobs(batches[0][0])
-        nc.vector.scalar_tensor_tensor(
-            out=shift_sb[:], in0=mean_sb[:], scalar=-1.0, in1=rstd_sb[:], op0=ALU.mult, op1=ALU.mult
-        )
+        gather("dve", *t1)
+        silu_h(0, 0)
         tanh_h(0, 1)
         silu_h(0, 1)
+        quant_grad(0, 1)
+        mm(0, 2)
+        copies = run_jobs(g_jobs[0:2])
 
-        pending = []
+        pending = g_jobs[0:2]
         for k in range(7):
             first = k == 0
             b1, b2, b3 = batches[k]
             on_act = NORM_ACT[k]
-            for ld in early_loads.get(k, []):
-                ld()
             if k + 2 < 8:
                 load_h(k + 2, 0)
-                load_y(k + 2)
+            for ld in early_loads.get(k, []):
+                ld()
+            negate_mean(k, 0)
             gate_da(k, 0)
+            norm_y(k, 0, "pool")
+            norm_y(k, 1, "pool")
             if not first:
                 sum_frames(k - 1, SCALE)
-            norm_y(k, 0)
             gate_da(k, 1)
-            if first:
-                quant_grad(0, 1)
-                mm(0, 2)
-            norm_y(k, 1)
+            gate_da(k, 2)
             mm(k, 3)
             silu_h(k + 1, 0)
-            if not first:
+            if first:
+                finish(copies)
+            else:
                 de_shift(k - 1)
                 gain_term(k - 1)
-            if not first:
-                copies = run_jobs(b1)
+            make_dh(k, 0)
+            copies = run_jobs(b1)
             tanh_h(k + 1, 0)
+            silu_h(k + 1, 1)
             finish(copies)
-            for f in on_act:
-                norm_y(k, f, "act")
             if k + 2 < 8:
                 load_h(k + 2, 1)
-            make_dh(k, 0)
             quant_done(pending)
-            if first:
-                nc.vector.tensor_scalar(out=gb[:], in0=gb_raw[:, :, 0:8], scalar1=0.25, scalar2=None, op0=ALU.mult)
-            if k == 3:
-                quant_emb(0)
-            if k == 4:
-                quant_emb(1)
+            mm(k + 1, 0)
+            if k in (3, 4):
+                quant_emb(k - 3)
             for ld in extra_loads.get(k, []):
                 ld()
+            make_prod(k, 0)
+            negate_mean(k, 1)
+            gate_da(k, 3)
+            norm_y(k, 2, "pool")
+            norm_y(k, 3, "dve" if first else "pool")
             if not first:
                 de_scale(k - 1)
-            make_prod(k, 0)
+            outs = [out0_mm(0, n, ("s1", "s0")[n]) for n in (0, 1)] if k == 6 else []
+            copies = run_jobs(b2)
+            for n, ps in enumerate(outs):
+                out0_gate(0, n, ps)
             if not first:
                 weave_de(k - 1)
-            outs = [out0_mm(0, n, ("s1", "s0")[n]) for n in (0, 1)] if k == 6 else []
-            gate_da(k, 2)
             quant_done(b1)
-            mm(k + 1, 0)
-            copies = run_jobs(b2)
-            silu_h(k + 1, 1)
+            mm(k + 1, 1)
+            tanh_h(k + 1, 1)
             finish(copies)
             for ld in late_loads.get(k, []):
                 ld()
-            if 2 not in on_act:
-                norm_y(k, 2)
-            gate_da(k, 3)
-            if not first:
-                quant_de_f(k - 1)
-            if 3 not in on_act:
-                norm_y(k, 3)
-            for n, ps in enumerate(outs):
-                out0_gate(0, n, ps)
-            mm(k + 1, 1)
-            copies = run_jobs(b3)
-            tanh_h(k + 1, 1)
-            finish(copies)
+            if k + 2 < 8:
+                load_y(k + 2)
+            if first:
+                nc.vector.tensor_scalar(out=gb[:], in0=gb_raw[:, :, 0:8], scalar1=0.25, scalar2=None, op0=ALU.mult)
+            finish(run_jobs(b3))
+            mm(k + 1, 2)
             if k in (2, 3):
                 silu_emb(k - 2)
             if k == 5:
                 emb_acts(0)
             make_dh(k, 1)
+            if not first:
+                quant_de_f(k - 1)
             quant_done(b2)
             if outs:
                 out0_end(0)
-                load_emb_rows(2)
-            mm(k + 1, 2)
             sum_frames(k, SHIFT)
             make_prod(k, 1)
             if k == 6:
@@ -564,43 +571,45 @@ def tile_temporalcrossattention_pa_v_kernel(
             pending = b3
 
         load_emb_rows(3)
+        negate_mean(7, 0)
         gate_da(7, 0)
+        norm_y(7, 0, "pool")
+        norm_y(7, 1, "pool")
         sum_frames(6, SCALE)
         gate_da(7, 1)
         mm(7, 3)
-        norm_y(7, 0, "act")
         de_shift(6)
         gain_term(6)
-        norm_y(7, 1, "act")
+        finish(run_jobs(batches[7][0]))
         gate_da(7, 2)
         make_dh(7, 0)
-        gate_da(7, 3)
-        de_scale(6)
-        make_dh(7, 1)
         outs = [out0_mm(1, n, "da") for n in (0, 1)]
-        norm_y(7, 2, "act")
-        norm_y(7, 3, "act")
+        emb_acts(2)
+        negate_mean(7, 1)
+        gate_da(7, 3)
+        norm_y(7, 2, "pool")
+        norm_y(7, 3, "pool")
+        de_scale(6)
+        out0_gate(1, 0, outs[0])
+        make_dh(7, 1)
         sum_frames(7, SHIFT)
-        emb_tanh(2)
         make_prod(7, 0)
         make_prod(7, 1)
         de_shift(7)
-        copies = run_jobs(batches[7][0])
         t0 = turn_de(1, SHIFT, 0, "misc")
         t1 = turn_de(1, SHIFT, 1, "da")
         sum_frames(7, SCALE)
-        finish(copies)
-        for n, ps in enumerate(outs):
-            out0_gate(1, n, ps)
+        out0_gate(1, 1, outs[1])
+        weave_de(6)
+        emb_tanh(3)
         gather("act", *t0)
         gather("dve", *t1)
-        emb_silu(2)
-        weave_de(6)
+        quant_de_f(6)
         quant_de_b(1, SHIFT)
+        emb_silu(3)
         gain_term(7)
         out0_end(1)
         de_scale(7)
-        quant_de_f(6)
         tags = ("misc", "da")
         for m in range(4):
             out1_copy("act", 1, SHIFT, m, out1_mm(SHIFT, m, tags[m % 2]))
@@ -612,22 +621,20 @@ def tile_temporalcrossattention_pa_v_kernel(
             out1_copy("act", 1, SHIFT, m, out1_mm(SHIFT, m, tags[m % 2]))
         weave_de(7)
         quant_de_b(1, SCALE)
-        outs = [out0_mm(2, n, ("s0", "s1")[n]) for n in (0, 1)]
-        quant_de_f(7)
-        for n, ps in enumerate(outs):
-            out0_gate(2, n, ps)
-        emb_tanh(3)
+        ps = out0_mm(2, 0, "s0")
         for m in range(0, 2):
-            out1_copy("dve", 1, SCALE, m, out1_mm(SCALE, m, tags[m % 2]))
+            out1_copy("act", 1, SCALE, m, out1_mm(SCALE, m, tags[m % 2]))
+        quant_de_f(7)
+        out0_gate(2, 0, ps)
+        out0_gate(2, 1, out0_mm(2, 1, "s1"))
         for m in range(2, 4):
             out1_copy("act", 1, SCALE, m, out1_mm(SCALE, m, tags[m % 2]))
-        out0_end(2)
         outs = [out0_mm(3, n, ("s0", "s1")[n]) for n in (0, 1)]
-        emb_silu(3)
+        out0_end(2)
         for n, ps in enumerate(outs):
             out0_gate(3, n, ps)
         for m in range(4, 6):
             out1_copy("act", 1, SCALE, m, out1_mm(SCALE, m, tags[m % 2]))
+        out1_copy("dve", 1, SCALE, 6, out1_mm(SCALE, 6, "misc"))
         out0_end(3)
-        out1_copy("act", 1, SCALE, 6, out1_mm(SCALE, 6, "misc"))
-        out1_copy("dve", 1, SCALE, 7, out1_mm(SCALE, 7, "da"))
+        out1_copy("act", 1, SCALE, 7, out1_mm(SCALE, 7, "da"))

@@ -314,7 +314,10 @@ def tile_temporalcrossattention_pa_v_kernel(
         def weave_de(k):
             half, c = divmod(k, 4)
             gis[k] = work.tile([P, 2, P, 4], BF16, name="gi", tag="gi", bufs=2, align_bytes=64)
-            nc.vector.tensor_copy(out=gis[k][:], in_=des[half][:, :, :, P * c : P * (c + 1)].rearrange("p a t q -> p a q t"))
+            nc.vector.tensor_copy(
+                out=gis[k][:].rearrange("p a (r i) t -> p a r t i", i=4),
+                in_=des[half][:, :, :, P * c : P * (c + 1)].rearrange("p a t (r i) -> p a r t i", i=4),
+            )
 
         def quant_de_f(k):
             quant(gis[k][:].rearrange("p a q t -> p (a q t)"), df_mx, 256 * k, 256, E5)
@@ -442,11 +445,11 @@ def tile_temporalcrossattention_pa_v_kernel(
         load_wo(0, 0)
         load_wo(0, 1)
         load_grad(0, 0)
-        load_h(0, 0)
         load_grad(0, 1)
+        load_h(0, 0)
         load_stats()
-        load_y(0)
         load_h(0, 1)
+        load_y(0)
         load_grad(1, 0)
         load_h(1, 0)
         load_grad(1, 1)
@@ -471,20 +474,19 @@ def tile_temporalcrossattention_pa_v_kernel(
         quant_wo(0, 0)
         gather("act", *t0)
         quant_wo(0, 1)
-        gather("dve", *t1)
-        tanh_h(0, 0)
-        keep_clock(KEEP)
+        gather("act", *t1)
         t0 = turn_grad(0, 2)
         t1 = turn_grad(0, 3)
+        tanh_h(0, 0)
+        gather("dve", *t0)
         quant_grad(0, 0)
+        gather("dve", *t1)
         load_grad(2, 0)
         load_y(1)
         load_grad(2, 1)
         load_gain_bias()
         mm(0, 0)
         mm(0, 1)
-        gather("act", *t0)
-        gather("dve", *t1)
         silu_h(0, 0)
         tanh_h(0, 1)
         silu_h(0, 1)
@@ -492,6 +494,7 @@ def tile_temporalcrossattention_pa_v_kernel(
         mm(0, 2)
         copies = run_jobs(g_jobs[0:2])
 
+        negate_mean(0, 0)
         pending = g_jobs[0:2]
         for k in range(7):
             first = k == 0
@@ -501,7 +504,6 @@ def tile_temporalcrossattention_pa_v_kernel(
                 load_h(k + 2, 0)
             for ld in early_loads.get(k, []):
                 ld()
-            negate_mean(k, 0)
             gate_da(k, 0)
             norm_y(k, 0, "pool")
             norm_y(k, 1, "pool")
@@ -511,6 +513,7 @@ def tile_temporalcrossattention_pa_v_kernel(
             gate_da(k, 2)
             mm(k, 3)
             silu_h(k + 1, 0)
+            tanh_h(k + 1, 0)
             if first:
                 finish(copies)
             else:
@@ -518,7 +521,6 @@ def tile_temporalcrossattention_pa_v_kernel(
                 gain_term(k - 1)
             make_dh(k, 0)
             copies = run_jobs(b1)
-            tanh_h(k + 1, 0)
             silu_h(k + 1, 1)
             finish(copies)
             if k + 2 < 8:
@@ -529,8 +531,8 @@ def tile_temporalcrossattention_pa_v_kernel(
                 quant_emb(k - 3)
             for ld in extra_loads.get(k, []):
                 ld()
-            make_prod(k, 0)
             negate_mean(k, 1)
+            make_prod(k, 0)
             gate_da(k, 3)
             norm_y(k, 2, "pool")
             norm_y(k, 3, "dve" if first else "pool")
@@ -565,13 +567,13 @@ def tile_temporalcrossattention_pa_v_kernel(
             if outs:
                 out0_end(0)
             sum_frames(k, SHIFT)
+            negate_mean(k + 1, 0)
             make_prod(k, 1)
             if k == 6:
                 emb_acts(1)
             pending = b3
 
         load_emb_rows(3)
-        negate_mean(7, 0)
         gate_da(7, 0)
         norm_y(7, 0, "pool")
         norm_y(7, 1, "pool")
@@ -582,10 +584,10 @@ def tile_temporalcrossattention_pa_v_kernel(
         gain_term(6)
         finish(run_jobs(batches[7][0]))
         gate_da(7, 2)
+        negate_mean(7, 1)
         make_dh(7, 0)
         outs = [out0_mm(1, n, "da") for n in (0, 1)]
         emb_acts(2)
-        negate_mean(7, 1)
         gate_da(7, 3)
         norm_y(7, 2, "pool")
         norm_y(7, 3, "pool")

@@ -18,15 +18,13 @@ ALU = mybir.AluOpType
 
 P = 128
 N = 512
+UNITS = 8
+LAST = UNITS - 1
 SCALE, SHIFT = 0, 1
-NORM_ACT = ((), (), (), (), (), (), ())
-ON_DVE = (("g", 1, 0), ("g", 1, 1))
-WARM = 5
-LAST = "pool"
-FILL = 0
-RAW = 3
-ET = 1
-KEEP = 1
+
+BANKS = {"da": 3, "sum_shift": 1, "sum_scale": 1, "side": 3}
+
+BATCHES = ((2, 2, 2), (2, 2, 2), (2, 2, 2), (3, 3, 2), (2, 2, 2), (2, 3, 3), (3, 2, 3))
 
 
 def tile_temporalcrossattention_pa_v_kernel(
@@ -39,408 +37,391 @@ def tile_temporalcrossattention_pa_v_kernel(
         psum = ctx.enter_context(tc.psum_pool(name="psum", bufs=1))
         ctx.enter_context(tc.manual_schedule())
 
-        def mx_pair(name, width):
+        def mx_operand(name, width):
             codes = keep.tile([P, width], U32, name=name + "_codes", align_bytes=64)
             scales = keep.tile([P, width], U8, name=name + "_scales", align_bytes=64)
             return codes, scales
 
-        g_mx = mx_pair("grad", 4096)
-        wo_mx = mx_pair("wo", 2048)
-        we_mx = mx_pair("we", 4096)
-        e_mx = mx_pair("emb", 1024)
-        df_mx = mx_pair("de_f", 2048)
-        db_mx = mx_pair("de_b", 1024)
+        grad_mx = mx_operand("grad", 4096)
+        wo_mx = mx_operand("wo", 2048)
+        we_mx = mx_operand("we", 4096)
+        emb_mx = mx_operand("emb", 1024)
+        de_feat_mx = mx_operand("de_feat", 2048)
+        de_seq_mx = mx_operand("de_seq", 1024)
 
         ident = keep.tile([P, P], F32)
         make_identity(nc, ident[:])
         mean_sb = keep.tile([P, 2, 8], F32)
         rstd_sb = keep.tile([P, 2, 8], F32)
-        gb_raw = keep.tile([P, 2, 16], BF16)
-        gb = keep.tile([P, 2, 8], F32)
-        warm = keep.tile([P, N], BF16)
+        gain_bias_raw = keep.tile([P, 2, 16], BF16)
+        gain_bias = keep.tile([P, 2, 8], F32)
 
-        raws, grps, hs, ys, sil, tnh, prod, das, sums, xs, des, gis, ers, eas, stages, dhs, ets, negs = (
-            {}, {}, {}, {}, {}, {}, {}, {}, {}, {}, {}, {}, {}, {}, {}, {}, {}, {})
+        raw, staged, h_sb, y_sb, silu_sb, tanh_sb, neg_mean = {}, {}, {}, {}, {}, {}, {}
+        da, dh, prod, sums, gain_sum, de, woven = {}, {}, {}, {}, {}, {}, {}
+        emb_rows, emb_silu_sb, emb_tanh_sb, out1_sb = {}, {}, {}, {}
 
-        def seqs(c):
+        def sequences(c):
             u, hi = divmod(c, 2)
             return slice(256 * hi + u, 256 * (hi + 1), 2)
 
-        def cols(half):
-            return slice(N * half, N * (half + 1))
+        def span(i):
+            return slice(N * i, N * (i + 1))
 
         def raw_tile(key):
-            raws[key] = work.tile([P, 4096], BF16, name="raw", tag="raw", bufs=RAW, align_bytes=64)
-            return raws[key]
+            if key not in raw:
+                raw[key] = work.tile([P, 4096], BF16, name="raw", tag="raw", bufs=3, align_bytes=64)
+            return raw[key]
 
         def load_grad(c, pair):
-            key = ("g", c)
-            raw = raws[key] if key in raws else raw_tile(key)
             nc.sync.dma_start(
-                out=raw[:, 2048 * pair : 2048 * (pair + 1)],
-                in_=grad_out[seqs(c), 2 * pair : 2 * pair + 2, :].rearrange("q t k -> q (t k)"),
+                out=raw_tile(("grad", c))[:, 2048 * pair : 2048 * (pair + 1)],
+                in_=grad_out[sequences(c), 2 * pair : 2 * pair + 2, :].rearrange("q f k -> q (f k)"),
             )
 
-        def load_wo(half, pair):
-            key = ("wo", half)
-            raw = raws[key] if key in raws else raw_tile(key)
-            rows = Wo[cols(half), :].rearrange("(m t) k -> m (t k)", t=4)
-            nc.sync.dma_start(out=raw[:, 2048 * pair : 2048 * (pair + 1)], in_=rows[:, 2048 * pair : 2048 * (pair + 1)])
+        def load_wo(half, v):
+            rows = Wo[span(half), :].rearrange("(m t) k -> m (t k)", t=4)
+            piece = slice(2048 * v, 2048 * (v + 1))
+            nc.sync.dma_start(out=raw_tile(("wo", half))[:, piece], in_=rows[:, piece])
 
         def load_we(n, part):
-            raw = raw_tile(("we", n, part))
             nc.sync.dma_start(
-                out=raw[:].rearrange("p (a f) -> p a f", a=4),
-                in_=We[cols(n), D * part : D * (part + 1)].rearrange("(a p) f -> p a f", p=P),
+                out=raw_tile(("we", n, part))[:].rearrange("p (a f) -> p a f", a=4),
+                in_=We[span(n), D * part : D * (part + 1)].rearrange("(a p) f -> p a f", p=P),
             )
 
-        def load_emb():
-            raw = raw_tile("emb")
-            nc.sync.dma_start(out=raw[:], in_=emb0.rearrange("(p j) d -> p (j d)", j=4))
+        def load_emb(n):
+            raw["emb", n] = work.tile([P, 4, N], BF16, name="out1", tag="out1", bufs=3)
+            nc.sync.dma_start(out=raw["emb", n][:], in_=emb0.rearrange("(p j) d -> p j d", j=4)[:, :, span(n)])
 
         def load_emb_rows(c):
-            ers[c] = work.tile([P, D], BF16, name="er", tag="er", bufs=2)
-            nc.sync.dma_start(out=ers[c][:], in_=emb0[seqs(c), :])
+            emb_rows[c] = work.tile([P, D], BF16, name="emb_rows", tag="emb_rows", bufs=2)
+            nc.sync.dma_start(out=emb_rows[c][:], in_=emb0[sequences(c), :])
 
         def load_h(k, pair):
             half, c = divmod(k, 4)
-            hs[k, pair] = work.tile([P, 2, N], F32, name="hh", tag="hh", bufs=4)
-            nc.sync.dma_start(out=hs[k, pair][:], in_=h[seqs(c), 2 * pair : 2 * pair + 2, cols(half)])
+            h_sb[k, pair] = work.tile([P, 2, N], F32, name="h", tag="h", bufs=4)
+            nc.sync.dma_start(out=h_sb[k, pair][:], in_=h[sequences(c), 2 * pair : 2 * pair + 2, span(half)])
 
         def load_y(k):
             half, c = divmod(k, 4)
-            ys[k] = work.tile([P, T, N], BF16, name="yy", tag="yy", bufs=2)
-            nc.sync.dma_start(out=ys[k][:], in_=y[seqs(c), :, cols(half)])
+            y_sb[k] = work.tile([P, T, N], BF16, name="y", tag="y", bufs=2)
+            nc.sync.dma_start(out=y_sb[k][:], in_=y[sequences(c), :, span(half)])
 
         def load_stats():
-            nc.sync.dma_start(out=mean_sb[:], in_=mean.rearrange("(hi q u) t -> q hi (u t)", hi=2, u=2))
-            nc.sync.dma_start(out=rstd_sb[:], in_=rstd.rearrange("(hi q u) t -> q hi (u t)", hi=2, u=2))
+            nc.sync.dma_start(out=mean_sb[:], in_=mean.rearrange("(hi q u) f -> q hi (u f)", hi=2, u=2))
+            nc.sync.dma_start(out=rstd_sb[:], in_=rstd.rearrange("(hi q u) f -> q hi (u f)", hi=2, u=2))
 
         def load_gain_bias():
             for i, vec in enumerate((ln2_g, ln2_b)):
                 nc.sync.dma_start(
-                    out=gb_raw[:, i, 0:8].rearrange("p (a t) -> p a t", a=2),
-                    in_=vec.rearrange("(a p t) -> p a t", a=2, t=4),
+                    out=gain_bias_raw[:, i, 0:8].rearrange("m (half t) -> m half t", half=2),
+                    in_=vec.rearrange("(half m t) -> m half t", half=2, t=4),
                 )
 
-        def bank(tag):
-            depth = {"da": 3, "s0": 1, "s1": 1, "misc": 3}[tag]
-            return psum.tile([P, N], F32, name=tag, tag=tag, bufs=depth)
+        def bank(use):
+            return psum.tile([P, N], F32, name=use, tag=use, bufs=BANKS[use])
 
-        def copy_on(eng, out, in_):
-            if eng == "act":
-                nc.scalar.copy(out=out, in_=in_)
-            else:
-                nc.vector.tensor_copy(out=out, in_=in_)
+        def staging(key):
+            if key not in staged:
+                staged[key] = work.tile([P, 4 * N], BF16, name="staged", tag="staged", bufs=4, align_bytes=64)
+            return staged[key]
 
-        def grp_tile(key):
-            if key not in grps:
-                grps[key] = work.tile([P, 2048], BF16, name="grp", tag="grp", bufs=4, align_bytes=64)
-            return grps[key]
-
-        def turn(sources, tag="misc"):
-            ps = bank(tag)
-            for i, src in enumerate(sources):
-                nc.tensor.transpose(ps[:, P * i : P * (i + 1)], src, ident[:])
+        def turn(blocks, use):
+            ps = bank(use)
+            for i, block in enumerate(blocks):
+                nc.tensor.transpose(ps[:, P * i : P * (i + 1)], block, ident[:])
             return ps
 
-        def gather(eng, ps, key, slot):
-            words = grp_tile(key)[:].bitcast(F32)[:, N * slot : N * (slot + 1)]
-            copy_on(eng, words.rearrange("p (a m u) -> p a m u", a=2, u=2), ps[:].rearrange("p (a u m) -> p a m u", a=2, u=2))
-
-        def every_2nd(key, first):
-            words = raws[key][:].bitcast(F32)
-            return [words[:, w + u : w + 256 : 2] for w in first for u in (0, 1)]
+        def every_2nd_word(key, starts):
+            words = raw[key][:].bitcast(F32)
+            return [words[:, w + u : w + 256 : 2] for w in starts for u in (0, 1)]
 
         def turn_grad(c, f):
-            return turn(every_2nd(("g", c), (512 * f, 512 * f + 256))), ("g", c, f // 2), f % 2
+            return turn(every_2nd_word(("grad", c), (512 * f, 512 * f + 256)), "side"), ("grad", c, f // 2), f % 2
 
-        def turn_wo(half, g, pair):
-            return turn(every_2nd(("wo", half), (1024 * pair + 256 * g, 1024 * pair + 512 + 256 * g))), ("wo", half, g), pair
+        def turn_wo(half, g, v):
+            starts = (1024 * v + 256 * g, 1024 * v + 512 + 256 * g)
+            return turn(every_2nd_word(("wo", half), starts), "side"), ("wo", half, g), v
 
-        def turn_we(n, part, half, pair):
-            first = (1024 * pair + 256 * half, 1024 * pair + 512 + 256 * half)
-            return turn(every_2nd(("we", n, part), first)), ("we", n, part, half), pair
+        def turn_we(n, part, half, side):
+            starts = (1024 * side + 256 * half, 1024 * side + 512 + 256 * half)
+            return turn(every_2nd_word(("we", n, part), starts), "side"), ("we", n, part, half), side
 
-        def turn_de(half, part, pair, tag="misc"):
-            words = des[half][:].rearrange("p a t b -> p (a t b)").bitcast(F32)
-            first = [(4 * part + 2 * pair + a) * 256 + P * u for a in (0, 1) for u in (0, 1)]
-            return turn([words[:, w : w + P] for w in first], tag), ("de", half, part), pair
+        def turn_de(half, part, v, use="side"):
+            words = de[half][:].rearrange("m part t b -> m (part t b)").bitcast(F32)
+            starts = [(4 * part + 2 * v + e) * 256 + P * u for e in (0, 1) for u in (0, 1)]
+            return turn([words[:, w : w + P] for w in starts], use), ("de", half, part), v
 
-        def quant(src, mx, first, width, fmt):
+        def gather(engine, ps, key, side):
+            words = staging(key)[:].bitcast(F32)[:, span(side)].rearrange("p (a m u) -> p a m u", a=2, u=2)
+            src = ps[:].rearrange("p (a u m) -> p a m u", a=2, u=2)
+            if engine == "scalar":
+                nc.scalar.copy(out=words, in_=src)
+            else:
+                nc.vector.tensor_copy(out=words, in_=src)
+
+        def quantise(src, operand, start, width, fmt):
+            codes, scales = operand
             nc.vector.quantize_mx(
-                out=mx[0][:, first : first + width].bitcast(fmt), scales=mx[1][:, first : first + width], in_=src
+                out=codes[:, start : start + width].bitcast(fmt), scales=scales[:, start : start + width], in_=src
             )
 
         def quant_grad(c, pair):
-            quant(grps["g", c, pair][:], g_mx, 1024 * c + N * pair, N, E5)
+            quantise(staged["grad", c, pair][:], grad_mx, 1024 * c + N * pair, N, E5)
 
         def quant_wo(half, g):
-            quant(grps["wo", half, g][:], wo_mx, 1024 * half + N * g, N, E4)
+            quantise(staged["wo", half, g][:], wo_mx, 1024 * half + N * g, N, E4)
 
         def quant_we(n, part, half):
-            quant(grps["we", n, part, half][:], we_mx, 2048 * part + 1024 * half + N * n, N, E4)
+            quantise(staged["we", n, part, half][:], we_mx, 2048 * part + 1024 * half + N * n, N, E4)
 
-        def quant_de_b(half, part):
-            quant(grps["de", half, part][:], db_mx, N * part, N, E5)
+        def quant_de_seq(half, part):
+            quantise(staged["de", half, part][:], de_seq_mx, N * part, N, E5)
 
-        def mx(ps, lhs, l0, lfmt, rhs, r0, rfmt, start, stop):
+        def quant_emb(n):
+            quantise(staged["emb", n][:], emb_mx, N * n, N, E4)
+
+        def mx_pass(ps, lhs, lhs_at, lhs_fmt, rhs, rhs_at, rhs_fmt, start, stop):
             nc.tensor.matmul_mx(
                 out=ps[:],
-                lhsT=lhs[0][:, l0 : l0 + P].bitcast(lfmt),
-                lhsT_scale=lhs[1][:, l0 : l0 + P],
-                rhs=rhs[0][:, r0 : r0 + N].bitcast(rfmt),
-                rhs_scale=rhs[1][:, r0 : r0 + N],
+                lhsT=lhs[0][:, lhs_at : lhs_at + P].bitcast(lhs_fmt),
+                lhsT_scale=lhs[1][:, lhs_at : lhs_at + P],
+                rhs=rhs[0][:, rhs_at : rhs_at + N].bitcast(rhs_fmt),
+                rhs_scale=rhs[1][:, rhs_at : rhs_at + N],
                 start=start,
                 stop=stop,
             )
 
-        def mm(k, f):
+        def multiply_da(k, f):
             half, c = divmod(k, 4)
-            das[k, f] = bank("da")
+            da[k, f] = bank("da")
             for g in (0, 1):
-                mx(das[k, f], g_mx, 1024 * c + 256 * f + P * g, E5, wo_mx, 1024 * half + N * g, E4, g == 0, g == 1)
+                mx_pass(da[k, f], grad_mx, 1024 * c + 256 * f + P * g, E5, wo_mx, 1024 * half + N * g, E4, g == 0, g == 1)
 
-        def sorted_h(k, pair):
-            return hs[k, pair][:].rearrange("p f (j e) -> p f e j", e=2)
+        def activate_h(k, pair, into, name, func, scale):
+            into[k, pair] = work.tile([P, 2 * N], F32, name=name, tag=name, bufs=3)
+            nc.scalar.activation(
+                out=into[k, pair][:].rearrange("q (f e j) -> q f e j", f=2, e=2),
+                in_=h_sb[k, pair][:].rearrange("q f (j e) -> q f e j", e=2),
+                func=func,
+                scale=scale,
+            )
 
         def silu_h(k, pair):
-            sil[k, pair] = work.tile([P, 2 * N], F32, name="sil", tag="sil", bufs=3)
-            out = sil[k, pair][:].rearrange("p (f e j) -> p f e j", f=2, e=2)
-            nc.scalar.activation(out=out, in_=sorted_h(k, pair), func=ACT.Silu, scale=-1.0)
+            activate_h(k, pair, silu_sb, "silu", ACT.Silu, -1.0)
 
         def tanh_h(k, pair):
-            tnh[k, pair] = work.tile([P, 2 * N], F32, name="tnh", tag="tnh", bufs=3)
-            out = tnh[k, pair][:].rearrange("p (f e j) -> p f e j", f=2, e=2)
-            nc.scalar.activation(out=out, in_=sorted_h(k, pair), func=ACT.Tanh, scale=0.5)
+            activate_h(k, pair, tanh_sb, "tanh", ACT.Tanh, 0.5)
 
         def gate_da(k, f):
             if f % 2 == 0:
-                dhs[k, f // 2] = work.tile([P, 2, 2, 256], F32, name="dh", tag="dh", bufs=4)
+                dh[k, f // 2] = work.tile([P, 2, 2, 256], F32, name="dh", tag="dh", bufs=4)
             nc.vector.scalar_tensor_tensor(
-                out=dhs[k, f // 2][:, :, f % 2, :],
-                in0=tnh[k, f // 2][:, cols(f % 2)].rearrange("p (r v) -> p v r", v=2),
+                out=dh[k, f // 2][:, :, f % 2, :],
+                in0=tanh_sb[k, f // 2][:, span(f % 2)].rearrange("q (r v) -> q v r", v=2),
                 scalar=1.0,
-                in1=das[k, f][:].rearrange("p (v r) -> p v r", v=2),
+                in1=da[k, f][:].rearrange("q (v r) -> q v r", v=2),
                 op0=ALU.add,
                 op1=ALU.mult,
             )
 
-        def norm_y(k, f, eng="dve"):
-            c = k % 4
-            u, hi = divmod(c, 2)
-            if (k, f // 2) not in prod:
-                prod[k, f // 2] = work.tile([P, 2, 2, 256], F32, name="prod", tag="prod", bufs=3)
-            j = 4 * u + f
-            if eng == "pool":
-                nc.gpsimd.tensor_scalar(
-                    out=prod[k, f // 2][:, :, f % 2, :].rearrange("p v (e m) -> p v e m", e=2),
-                    in0=ys[k][:, f, :].rearrange("p (m v e) -> p v e m", v=2, e=2),
-                    scalar1=negs[k, f // 2][:, f % 2 : f % 2 + 1],
-                    scalar2=rstd_sb[:, hi, j : j + 1],
-                    op0=ALU.add,
-                    op1=ALU.mult,
-                )
-                return
-            nc.vector.tensor_scalar(
-                out=prod[k, f // 2][:, :, f % 2, :].rearrange("p v (e m) -> p v e m", e=2),
-                in0=ys[k][:, f, :].rearrange("p (m v e) -> p v e m", v=2, e=2),
-                scalar1=mean_sb[:, hi, j : j + 1],
-                scalar2=rstd_sb[:, hi, j : j + 1],
-                op0=ALU.subtract,
-                op1=ALU.mult,
-            )
+        def finish_dh(k, pair):
+            both = dh[k, pair][:].rearrange("q v f r -> q v (f r)")
+            silu = silu_sb[k, pair][:].rearrange("q (r v) -> q v r", v=2)
+            nc.vector.scalar_tensor_tensor(out=both, in0=silu, scalar=1.0, in1=both, op0=ALU.subtract, op1=ALU.mult)
 
         def negate_mean(k, pair):
             u, hi = divmod(k % 4, 2)
             j = 4 * u + 2 * pair
-            negs[k, pair] = work.tile([P, 2], F32, name="neg", tag="neg", bufs=4)
+            neg_mean[k, pair] = work.tile([P, 2], F32, name="neg_mean", tag="neg_mean", bufs=4)
             nc.vector.tensor_scalar(
-                out=negs[k, pair][:], in0=mean_sb[:, hi, j : j + 2], scalar1=-1.0, scalar2=None, op0=ALU.mult
+                out=neg_mean[k, pair][:], in0=mean_sb[:, hi, j : j + 2], scalar1=-1.0, scalar2=None, op0=ALU.mult
             )
 
-        def make_dh(k, pair):
-            dh = dhs[k, pair][:].rearrange("p v f r -> p v (f r)")
-            a = sil[k, pair][:].rearrange("p (r v) -> p v r", v=2)
-            nc.vector.scalar_tensor_tensor(out=dh, in0=a, scalar=1.0, in1=dh, op0=ALU.subtract, op1=ALU.mult)
+        def normalise(k, f, engine=nc.gpsimd):
+            u, hi = divmod(k % 4, 2)
+            if f % 2 == 0:
+                prod[k, f // 2] = work.tile([P, 2, 2, 256], F32, name="prod", tag="prod", bufs=3)
+            engine.tensor_scalar(
+                out=prod[k, f // 2][:, :, f % 2, :].rearrange("q v (e m) -> q v e m", e=2),
+                in0=y_sb[k][:, f, :].rearrange("q (m v e) -> q v e m", v=2, e=2),
+                scalar1=neg_mean[k, f // 2][:, f % 2 : f % 2 + 1],
+                scalar2=rstd_sb[:, hi, 4 * u + f : 4 * u + f + 1],
+                op0=ALU.add,
+                op1=ALU.mult,
+            )
 
-        def make_prod(k, pair):
-            p = prod[k, pair][:]
-            nc.vector.tensor_tensor(out=p, in0=p, in1=dhs[k, pair][:], op=ALU.mult)
+        def finish_prod(k, pair):
+            both = prod[k, pair][:]
+            nc.vector.tensor_tensor(out=both, in0=both, in1=dh[k, pair][:], op=ALU.mult)
 
         def sum_frames(k, part):
-            src = prod if part == SCALE else dhs
-            ps = bank("s1" if part == SCALE else "s0")
-            sums[k, part] = ps
+            src = prod if part == SCALE else dh
+            sums[k, part] = bank("sum_scale" if part == SCALE else "sum_shift")
             for t in range(4):
                 for f in range(T):
-                    block = src[k, f // 2][:, t // 2, f % 2, P * (t % 2) : P * (t % 2 + 1)]
                     nc.tensor.matmul(
-                        ps[:, P * t : P * (t + 1)], lhsT=block, rhs=ident[:],
-                        start=(f == 0), stop=(f == T - 1), is_transpose=True,
+                        sums[k, part][:, P * t : P * (t + 1)],
+                        lhsT=src[k, f // 2][:, t // 2, f % 2, P * (t % 2) : P * (t % 2 + 1)],
+                        rhs=ident[:],
+                        start=(f == 0),
+                        stop=(f == T - 1),
+                        is_transpose=True,
                     )
-
-        def de_tile(half):
-            if half not in des:
-                des[half] = work.tile([P, 2, 4, B], BF16, name="de", tag="de", bufs=2, align_bytes=64)
-            return des[half]
 
         def de_shift(k):
             half, c = divmod(k, 4)
+            if c == 0:
+                de[half] = work.tile([P, 2, 4, B], BF16, name="de", tag="de", bufs=2, align_bytes=64)
             nc.scalar.activation(
-                out=de_tile(half)[:, SHIFT, :, P * c : P * (c + 1)],
-                in_=sums[k, SHIFT][:].rearrange("p (t q) -> p t q", t=4), func=ACT.Copy, scale=0.25,
+                out=de[half][:, SHIFT, :, P * c : P * (c + 1)],
+                in_=sums[k, SHIFT][:].rearrange("m (t q) -> m t q", t=4),
+                func=ACT.Copy,
+                scale=0.25,
             )
 
-        def gain_term(k):
-            half = k // 4
-            xs[k] = work.tile([P, N], F32, name="xs", tag="xs", bufs=1)
+        def apply_gain(k):
+            gain_sum[k] = work.tile([P, N], F32, name="gain_sum", tag="gain_sum", bufs=1)
             for t in range(4):
+                j = 4 * (k // 4) + t
                 nc.scalar.activation(
-                    out=xs[k][:, P * t : P * (t + 1)], in_=sums[k, SCALE][:, P * t : P * (t + 1)],
-                    func=ACT.Copy, scale=gb[:, 0, 4 * half + t : 4 * half + t + 1],
+                    out=gain_sum[k][:, P * t : P * (t + 1)],
+                    in_=sums[k, SCALE][:, P * t : P * (t + 1)],
+                    func=ACT.Copy,
+                    scale=gain_bias[:, 0, j : j + 1],
                 )
 
         def de_scale(k):
             half, c = divmod(k, 4)
             for t in range(4):
+                j = 4 * half + t
                 nc.vector.scalar_tensor_tensor(
-                    out=de_tile(half)[:, SCALE, t, P * c : P * (c + 1)],
+                    out=de[half][:, SCALE, t, P * c : P * (c + 1)],
                     in0=sums[k, SHIFT][:, P * t : P * (t + 1)],
-                    scalar=gb[:, 1, 4 * half + t : 4 * half + t + 1],
-                    in1=xs[k][:, P * t : P * (t + 1)], op0=ALU.mult, op1=ALU.add,
+                    scalar=gain_bias[:, 1, j : j + 1],
+                    in1=gain_sum[k][:, P * t : P * (t + 1)],
+                    op0=ALU.mult,
+                    op1=ALU.add,
                 )
 
         def weave_de(k):
             half, c = divmod(k, 4)
-            gis[k] = work.tile([P, 2, P, 4], BF16, name="gi", tag="gi", bufs=2, align_bytes=64)
+            woven[k] = work.tile([P, 2, P, 4], BF16, name="woven", tag="woven", bufs=2, align_bytes=64)
             nc.vector.tensor_copy(
-                out=gis[k][:].rearrange("p a (r i) t -> p a r t i", i=4),
-                in_=des[half][:, :, :, P * c : P * (c + 1)].rearrange("p a t (r i) -> p a r t i", i=4),
+                out=woven[k][:].rearrange("m part (r i) t -> m part r t i", i=4),
+                in_=de[half][:, :, :, P * c : P * (c + 1)].rearrange("m part t (r i) -> m part r t i", i=4),
             )
 
-        def quant_de_f(k):
-            quant(gis[k][:].rearrange("p a q t -> p (a q t)"), df_mx, 256 * k, 256, E5)
+        def quant_de_feat(k):
+            quantise(woven[k][:].rearrange("m part q t -> m (part q t)"), de_feat_mx, 256 * k, 256, E5)
 
         def silu_emb(n):
-            src = raws["emb"][:].rearrange("p (e u d) -> p d u e", e=2, u=2)[:, cols(n), :, :]
-            out = grp_tile(("e", n))[:].rearrange("p (d u e) -> p d u e", u=2, e=2)
-            nc.scalar.activation(out=out, in_=src, func=ACT.Silu)
-
-        def quant_emb(n):
-            quant(grps["e", n][:], e_mx, N * n, N, E4)
+            nc.scalar.activation(
+                out=staging(("emb", n))[:].rearrange("p (d u e) -> p d u e", u=2, e=2),
+                in_=raw["emb", n][:].rearrange("p (e u) d -> p d u e", e=2),
+                func=ACT.Silu,
+            )
 
         def emb_tanh(c):
-            tag, depth = ("et", 1) if c == 0 else ("tnh", 3)
-            ets[c] = work.tile([P, D], F32, name=tag, tag=tag, bufs=depth)
-            nc.scalar.activation(out=ets[c][:], in_=ers[c][:], func=ACT.Tanh, scale=0.5)
+            name, depth = ("emb_tanh", 1) if c == 0 else ("tanh", 3)
+            emb_tanh_sb[c] = work.tile([P, D], F32, name=name, tag=name, bufs=depth)
+            nc.scalar.activation(out=emb_tanh_sb[c][:], in_=emb_rows[c][:], func=ACT.Tanh, scale=0.5)
 
         def emb_silu(c):
-            tag, depth = ("ea", 2) if c < 2 else ("sil", 3)
-            eas[c] = work.tile([P, D], F32, name=tag, tag=tag, bufs=depth)
-            nc.scalar.activation(out=eas[c][:], in_=ers[c][:], func=ACT.Silu, scale=-1.0)
+            name, depth = ("emb_silu", 2) if c < 2 else ("silu", 3)
+            emb_silu_sb[c] = work.tile([P, D], F32, name=name, tag=name, bufs=depth)
+            nc.scalar.activation(out=emb_silu_sb[c][:], in_=emb_rows[c][:], func=ACT.Silu, scale=-1.0)
 
-        def emb_acts(c):
-            emb_tanh(c)
-            emb_silu(c)
-
-        def out0_mm(c, n, tag="misc"):
-            ps = bank(tag)
+        def multiply_out0(c, n, use):
+            ps = bank(use)
             passes = [(half, part) for half in (0, 1) for part in (SHIFT, SCALE)]
             for i, (half, part) in enumerate(passes):
-                mx(ps, df_mx, 256 * (4 * half + c) + P * part, E5, we_mx, 2048 * part + 1024 * half + N * n, E4, i == 0, i == 3)
+                de_at = 256 * (4 * half + c) + P * part
+                mx_pass(ps, de_feat_mx, de_at, E5, we_mx, 2048 * part + 1024 * half + N * n, E4, i == 0, i == 3)
             return ps
 
-        def out0_gate(c, n, ps):
-            part = ets[c][:, cols(n)]
-            nc.vector.scalar_tensor_tensor(out=part, in0=part, scalar=1.0, in1=ps[:], op0=ALU.add, op1=ALU.mult)
+        def gate_out0(c, n, ps):
+            cols = emb_tanh_sb[c][:, span(n)]
+            nc.vector.scalar_tensor_tensor(out=cols, in0=cols, scalar=1.0, in1=ps[:], op0=ALU.add, op1=ALU.mult)
 
-        def out0_end(c):
-            ea, et = eas[c], ets[c]
-            nc.vector.scalar_tensor_tensor(out=ea[:], in0=ea[:], scalar=1.0, in1=et[:], op0=ALU.subtract, op1=ALU.mult)
-            nc.sync.dma_start(out=out_0[seqs(c), :], in_=ea[:])
+        def store_out0(c):
+            rows = emb_silu_sb[c][:]
+            nc.vector.scalar_tensor_tensor(
+                out=rows, in0=rows, scalar=1.0, in1=emb_tanh_sb[c][:], op0=ALU.subtract, op1=ALU.mult
+            )
+            nc.sync.dma_start(out=out_0[sequences(c), :], in_=rows)
 
-        def out1_mm(part, m, tag="misc"):
-            ps = bank(tag)
-            mx(ps, e_mx, P * m, E4, db_mx, N * part, E5, True, True)
+        def multiply_out1(part, i, use):
+            ps = bank(use)
+            mx_pass(ps, emb_mx, P * i, E4, de_seq_mx, N * part, E5, True, True)
             return ps
 
-        def out1_copy(eng, half, part, m, ps):
-            key = (half, part, m // 2)
-            if key not in stages:
-                if half == 1 and m % 4 < 2:
-                    stages[key] = work.tile([P, 2, N], F32, name="hh", tag="hh", bufs=4)
-                else:
-                    stages[key] = work.tile([P, 2, N], F32, name="stage", tag="stage", bufs=3)
-            out = stages[key][:, m % 2, :].rearrange("p (r t) -> p r t", t=4)
-            src = ps[:].rearrange("p (t r) -> p r t", t=4)
-            if eng == "act":
-                nc.scalar.activation(out=out, in_=src, func=ACT.Copy, scale=-2.0)
+        def store_out1(engine, half, part, i, ps):
+            key = (half, part, i // 2)
+            if i % 2 == 0:
+                name, depth = ("h", 4) if half == 1 and i % 4 == 0 else ("out1", 3)
+                out1_sb[key] = work.tile([P, 2, N], F32, name=name, tag=name, bufs=depth)
+            dst = out1_sb[key][:, i % 2, :].rearrange("p (m t) -> p m t", t=4)
+            src = ps[:].rearrange("p (t m) -> p m t", t=4)
+            if engine == "scalar":
+                nc.scalar.activation(out=dst, in_=src, func=ACT.Copy, scale=-2.0)
             else:
-                nc.vector.tensor_scalar(out=out, in0=src, scalar1=-2.0, scalar2=None, op0=ALU.mult)
-            if m % 2 == 1:
+                nc.vector.tensor_scalar(out=dst, in0=src, scalar1=-2.0, scalar2=None, op0=ALU.mult)
+            if i % 2 == 1:
                 f0 = D * part + N * half
-                rows = out_1[P * (m - 1) : P * (m + 1), f0 : f0 + N].rearrange("(a p) f -> p a f", p=P)
-                nc.sync.dma_start(out=rows, in_=stages[key][:])
+                rows = out_1[P * (i - 1) : P * (i + 1), f0 : f0 + N].rearrange("(a p) f -> p a f", p=P)
+                nc.sync.dma_start(out=rows, in_=out1_sb[key][:])
 
-        def job(kind, *a):
-            if kind == "out1":
-                ps = out1_mm(a[1], a[2])
-                eng = "dve" if (kind,) + a in ON_DVE else "act"
-                return lambda: out1_copy(eng, a[0], a[1], a[2], ps)
-            turned = {"g": turn_grad, "wo": turn_wo, "we": turn_we, "de": turn_de}[kind](*a)
-            eng = "dve" if (kind,) + a in ON_DVE else "act"
-            return lambda: gather(eng, *turned)
+        side_jobs = (
+            [("grad", c, f) for c in (1, 2, 3) for f in range(T)]
+            + [("wo", 1, g, v) for g in (0, 1) for v in (0, 1)]
+            + [("we", n, part, half, side) for n in (0, 1) for part in (0, 1) for half in (0, 1) for side in (0, 1)]
+            + [("de", 0, part, v) for part in (SHIFT, SCALE) for v in (0, 1)]
+            + [("out1", part, i) for part in (SHIFT, SCALE) for i in range(8)]
+        )
 
-        def run_jobs(jobs):
-            return [job(*j) for j in jobs]
-
-        def finish(copies):
-            for cp in copies:
-                cp()
-
-        we_jobs = [("we", n, part, half, pair) for n in (0, 1) for part in (0, 1) for half in (0, 1) for pair in (0, 1)]
-        o1_jobs = [("out1", 0, part, m) for part in (SHIFT, SCALE) for m in range(8)]
-        de_jobs = [("de", 0, part, pair) for part in (SHIFT, SCALE) for pair in (0, 1)]
-        g_jobs = [("g", c, f) for c in (1, 2, 3) for f in range(T)]
-        wo_jobs = [("wo", 1, g, pair) for g in (0, 1) for pair in (0, 1)]
-        batches = {
-            0: (g_jobs[2:4], g_jobs[4:6], g_jobs[6:8]),
-            1: (g_jobs[8:10], g_jobs[10:12], wo_jobs[0:2]),
-            2: (wo_jobs[2:4], we_jobs[0:2], we_jobs[2:4]),
-            3: (we_jobs[4:6], we_jobs[6:8], we_jobs[8:10]),
-            4: (we_jobs[10:13], we_jobs[13:16], de_jobs[0:2]),
-            5: (de_jobs[2:4], o1_jobs[0:3], o1_jobs[3:6]),
-            6: (o1_jobs[6:9], o1_jobs[9:11], o1_jobs[11:14]),
-            7: (o1_jobs[14:16], [], []),
-        }
-
-        def quant_done(jobs):
+        def take(count):
+            jobs = side_jobs[:count]
             for j in jobs:
-                if j[0] == "g" and j[2] % 2 == 1:
+                side_jobs.remove(j)
+            return jobs
+
+        def fill_banks(jobs):
+            turns = {"grad": turn_grad, "wo": turn_wo, "we": turn_we, "de": turn_de}
+            return [multiply_out1(*j[1:], "side") if j[0] == "out1" else turns[j[0]](*j[1:]) for j in jobs]
+
+        def empty_banks(jobs, filled, engine="scalar"):
+            for j, result in zip(jobs, filled):
+                if j[0] == "out1":
+                    store_out1(engine, 0, j[1], j[2], result)
+                else:
+                    gather(engine, *result)
+
+        def quantise_staged(jobs):
+            for j in jobs:
+                if j[0] == "grad" and j[2] % 2 == 1:
                     quant_grad(j[1], j[2] // 2)
                 if j[0] == "wo" and j[3] == 1:
                     quant_wo(j[1], j[2])
                 if j[0] == "we" and j[4] == 1:
                     quant_we(j[1], j[2], j[3])
                 if j[0] == "de" and j[3] == 1:
-                    quant_de_b(j[1], j[2])
+                    quant_de_seq(j[1], j[2])
 
-        early_loads = {
-            0: [lambda: load_grad(3, 0), lambda: load_grad(3, 1)],
-            1: [lambda: load_we(0, 0)],
-            3: [lambda: load_we(1, 0)],
-            4: [lambda: load_we(1, 1)],
-            6: [lambda: load_emb_rows(2)],
+        side_loads = {
+            (0, 0): [(load_grad, 3, 0), (load_grad, 3, 1)],
+            (0, 1): [(load_wo, 1, 0), (load_wo, 1, 1)],
+            (1, 0): [(load_emb, 0), (load_we, 0, 0)],
+            (1, 2): [(load_emb, 1), (load_we, 0, 1)],
+            (2, 1): [(load_we, 1, 0)],
+            (3, 0): [(load_we, 1, 1)],
+            (3, 1): [(load_emb_rows, 0), (load_emb_rows, 1)],
+            (5, 0): [(load_emb_rows, 2)],
         }
-        extra_loads = {
-            0: [lambda: load_wo(1, 0), lambda: load_wo(1, 1)],
-            2: [lambda: load_we(0, 1)],
-            4: [lambda: load_emb_rows(0), lambda: load_emb_rows(1)],
-        }
-        late_loads = {
-            1: [lambda: load_emb()],
-        }
+
+        def load_side(k, point):
+            for load in side_loads.get((k, point), []):
+                load[0](*load[1:])
 
         load_wo(0, 0)
         load_wo(0, 1)
@@ -455,188 +436,174 @@ def tile_temporalcrossattention_pa_v_kernel(
         load_grad(1, 1)
         load_h(1, 1)
 
-        nc.vector.memset(warm[:], 0.0)
-
-        def keep_clock(count):
-            spare = bank("s1")
-            for i in range(count):
-                nc.tensor.matmul(spare[:], lhsT=warm[:, 0:P], rhs=warm[:], start=True, stop=True)
-
-        keep_clock(WARM)
-        gather("dve", *turn_wo(0, 0, 0))
-        gather("act", *turn_wo(0, 1, 0))
-        keep_clock(KEEP)
-        gather("dve", *turn_wo(0, 0, 1))
-        gather("act", *turn_wo(0, 1, 1))
-        keep_clock(KEEP)
-        t0 = turn_grad(0, 0)
-        t1 = turn_grad(0, 1)
-        quant_wo(0, 0)
-        gather("act", *t0)
-        quant_wo(0, 1)
-        gather("act", *t1)
-        t0 = turn_grad(0, 2)
-        t1 = turn_grad(0, 3)
+        for v in (0, 1):
+            gather("vector", *turn_wo(0, 0, v))
+            gather("scalar", *turn_wo(0, 1, v))
+        turned = [turn_grad(0, f) for f in (0, 1)]
+        for g in (0, 1):
+            quant_wo(0, g)
+            gather("scalar", *turned[g])
+        turned = [turn_grad(0, f) for f in (2, 3)]
         tanh_h(0, 0)
-        gather("dve", *t0)
+        gather("vector", *turned[0])
         quant_grad(0, 0)
-        gather("dve", *t1)
+        gather("vector", *turned[1])
         load_grad(2, 0)
         load_y(1)
         load_grad(2, 1)
         load_gain_bias()
-        mm(0, 0)
-        mm(0, 1)
+        multiply_da(0, 0)
+        multiply_da(0, 1)
         silu_h(0, 0)
         tanh_h(0, 1)
         silu_h(0, 1)
         quant_grad(0, 1)
-        mm(0, 2)
-        copies = run_jobs(g_jobs[0:2])
-
+        multiply_da(0, 2)
+        waiting = take(2)
+        filled = fill_banks(waiting)
         negate_mean(0, 0)
-        pending = g_jobs[0:2]
-        for k in range(7):
-            first = k == 0
-            b1, b2, b3 = batches[k]
-            on_act = NORM_ACT[k]
-            if k + 2 < 8:
+
+        for k in range(LAST):
+            batch1, batch2, batch3 = [take(count) for count in BATCHES[k]]
+            has_out0 = k == LAST - 1
+            if k + 2 < UNITS:
                 load_h(k + 2, 0)
-            for ld in early_loads.get(k, []):
-                ld()
+            load_side(k, 0)
             gate_da(k, 0)
-            norm_y(k, 0, "pool")
-            norm_y(k, 1, "pool")
-            if not first:
+            normalise(k, 0)
+            normalise(k, 1)
+            if k > 0:
                 sum_frames(k - 1, SCALE)
             gate_da(k, 1)
             gate_da(k, 2)
-            mm(k, 3)
+            multiply_da(k, 3)
             silu_h(k + 1, 0)
             tanh_h(k + 1, 0)
-            if first:
-                finish(copies)
+            if k == 0:
+                empty_banks(waiting, filled, "vector")
             else:
                 de_shift(k - 1)
-                gain_term(k - 1)
-            make_dh(k, 0)
-            copies = run_jobs(b1)
+                apply_gain(k - 1)
+            finish_dh(k, 0)
+            filled = fill_banks(batch1)
             silu_h(k + 1, 1)
-            finish(copies)
-            if k + 2 < 8:
+            empty_banks(batch1, filled)
+            if k + 2 < UNITS:
                 load_h(k + 2, 1)
-            quant_done(pending)
-            mm(k + 1, 0)
-            if k in (3, 4):
-                quant_emb(k - 3)
-            for ld in extra_loads.get(k, []):
-                ld()
-            negate_mean(k, 1)
-            make_prod(k, 0)
-            gate_da(k, 3)
-            norm_y(k, 2, "pool")
-            norm_y(k, 3, "dve" if first else "pool")
-            if not first:
-                de_scale(k - 1)
-            outs = [out0_mm(0, n, ("s1", "s0")[n]) for n in (0, 1)] if k == 6 else []
-            copies = run_jobs(b2)
-            for n, ps in enumerate(outs):
-                out0_gate(0, n, ps)
-            if not first:
-                weave_de(k - 1)
-            quant_done(b1)
-            mm(k + 1, 1)
-            tanh_h(k + 1, 1)
-            finish(copies)
-            for ld in late_loads.get(k, []):
-                ld()
-            if k + 2 < 8:
-                load_y(k + 2)
-            if first:
-                nc.vector.tensor_scalar(out=gb[:], in0=gb_raw[:, :, 0:8], scalar1=0.25, scalar2=None, op0=ALU.mult)
-            finish(run_jobs(b3))
-            mm(k + 1, 2)
+            quantise_staged(waiting)
+            multiply_da(k + 1, 0)
             if k in (2, 3):
-                silu_emb(k - 2)
-            if k == 5:
-                emb_acts(0)
-            make_dh(k, 1)
-            if not first:
-                quant_de_f(k - 1)
-            quant_done(b2)
-            if outs:
-                out0_end(0)
+                quant_emb(k - 2)
+            load_side(k, 1)
+            negate_mean(k, 1)
+            finish_prod(k, 0)
+            gate_da(k, 3)
+            normalise(k, 2)
+            if k == 0:
+                normalise(k, 3, nc.vector)
+            else:
+                normalise(k, 3)
+                de_scale(k - 1)
+            if has_out0:
+                out0 = [multiply_out0(0, 0, "sum_scale"), multiply_out0(0, 1, "sum_shift")]
+            filled = fill_banks(batch2)
+            if has_out0:
+                gate_out0(0, 0, out0[0])
+            if k > 0:
+                weave_de(k - 1)
+            if has_out0:
+                gate_out0(0, 1, out0[1])
+            quantise_staged(batch1)
+            multiply_da(k + 1, 1)
+            tanh_h(k + 1, 1)
+            empty_banks(batch2, filled)
+            load_side(k, 2)
+            if k + 2 < UNITS:
+                load_y(k + 2)
+            if k == 0:
+                nc.vector.tensor_scalar(
+                    out=gain_bias[:], in0=gain_bias_raw[:, :, 0:8], scalar1=0.25, scalar2=None, op0=ALU.mult
+                )
+            empty_banks(batch3, fill_banks(batch3))
+            multiply_da(k + 1, 2)
+            if k in (1, 2):
+                silu_emb(k - 1)
+            if k == 4:
+                emb_tanh(0)
+                emb_silu(0)
+            finish_dh(k, 1)
+            if k > 0:
+                quant_de_feat(k - 1)
+            quantise_staged(batch2)
+            if has_out0:
+                store_out0(0)
             sum_frames(k, SHIFT)
             negate_mean(k + 1, 0)
-            make_prod(k, 1)
-            if k == 6:
-                emb_acts(1)
-            pending = b3
+            finish_prod(k, 1)
+            if has_out0:
+                emb_tanh(1)
+                emb_silu(1)
+            waiting = batch3
 
         load_emb_rows(3)
-        gate_da(7, 0)
-        norm_y(7, 0, "pool")
-        norm_y(7, 1, "pool")
-        sum_frames(6, SCALE)
-        gate_da(7, 1)
-        mm(7, 3)
-        de_shift(6)
-        gain_term(6)
-        finish(run_jobs(batches[7][0]))
-        gate_da(7, 2)
-        negate_mean(7, 1)
-        make_dh(7, 0)
-        outs = [out0_mm(1, n, "da") for n in (0, 1)]
-        emb_acts(2)
-        gate_da(7, 3)
-        norm_y(7, 2, "pool")
-        norm_y(7, 3, "pool")
-        de_scale(6)
-        out0_gate(1, 0, outs[0])
-        make_dh(7, 1)
-        sum_frames(7, SHIFT)
-        make_prod(7, 0)
-        make_prod(7, 1)
-        de_shift(7)
-        t0 = turn_de(1, SHIFT, 0, "misc")
-        t1 = turn_de(1, SHIFT, 1, "da")
-        sum_frames(7, SCALE)
-        out0_gate(1, 1, outs[1])
-        weave_de(6)
+        gate_da(LAST, 0)
+        normalise(LAST, 0)
+        normalise(LAST, 1)
+        sum_frames(LAST - 1, SCALE)
+        gate_da(LAST, 1)
+        multiply_da(LAST, 3)
+        de_shift(LAST - 1)
+        apply_gain(LAST - 1)
+        empty_banks(side_jobs, fill_banks(side_jobs))
+        gate_da(LAST, 2)
+        negate_mean(LAST, 1)
+        finish_dh(LAST, 0)
+        out0 = [multiply_out0(1, n, "da") for n in (0, 1)]
+        emb_tanh(2)
+        emb_silu(2)
+        gate_da(LAST, 3)
+        normalise(LAST, 2)
+        normalise(LAST, 3)
+        de_scale(LAST - 1)
+        gate_out0(1, 0, out0[0])
+        finish_dh(LAST, 1)
+        sum_frames(LAST, SHIFT)
+        finish_prod(LAST, 0)
+        finish_prod(LAST, 1)
+        de_shift(LAST)
+        turned = [turn_de(1, SHIFT, v) for v in (0, 1)]
+        sum_frames(LAST, SCALE)
+        weave_de(LAST - 1)
+        gate_out0(1, 1, out0[1])
         emb_tanh(3)
-        gather("act", *t0)
-        gather("dve", *t1)
-        quant_de_f(6)
-        quant_de_b(1, SHIFT)
+        gather("scalar", *turned[0])
+        gather("vector", *turned[1])
+        quant_de_feat(LAST - 1)
+        quant_de_seq(1, SHIFT)
         emb_silu(3)
-        gain_term(7)
-        out0_end(1)
-        de_scale(7)
-        tags = ("misc", "da")
-        for m in range(4):
-            out1_copy("act", 1, SHIFT, m, out1_mm(SHIFT, m, tags[m % 2]))
-        t0 = turn_de(1, SCALE, 0, "s0")
-        t1 = turn_de(1, SCALE, 1, "s1")
-        gather("dve", *t0)
-        gather("dve", *t1)
-        for m in range(4, 8):
-            out1_copy("act", 1, SHIFT, m, out1_mm(SHIFT, m, tags[m % 2]))
-        weave_de(7)
-        quant_de_b(1, SCALE)
-        ps = out0_mm(2, 0, "s0")
-        for m in range(0, 2):
-            out1_copy("act", 1, SCALE, m, out1_mm(SCALE, m, tags[m % 2]))
-        quant_de_f(7)
-        out0_gate(2, 0, ps)
-        out0_gate(2, 1, out0_mm(2, 1, "s1"))
-        for m in range(2, 4):
-            out1_copy("act", 1, SCALE, m, out1_mm(SCALE, m, tags[m % 2]))
-        outs = [out0_mm(3, n, ("s0", "s1")[n]) for n in (0, 1)]
-        out0_end(2)
-        for n, ps in enumerate(outs):
-            out0_gate(3, n, ps)
-        for m in range(4, 6):
-            out1_copy("act", 1, SCALE, m, out1_mm(SCALE, m, tags[m % 2]))
-        out1_copy("dve", 1, SCALE, 6, out1_mm(SCALE, 6, "misc"))
-        out0_end(3)
-        out1_copy("act", 1, SCALE, 7, out1_mm(SCALE, 7, "da"))
+        apply_gain(LAST)
+        store_out0(1)
+        de_scale(LAST)
+
+        def out1_tiles(engine, part, first, count):
+            for i in range(first, first + count):
+                store_out1(engine, 1, part, i, multiply_out1(part, i, ("side", "da")[i % 2]))
+
+        out1_tiles("scalar", SHIFT, 0, 4)
+        ps = multiply_out0(2, 0, "sum_scale")
+        turned = [turn_de(1, SCALE, 0, "sum_shift"), turn_de(1, SCALE, 1, "da")]
+        gate_out0(2, 0, ps)
+        gather("vector", *turned[0])
+        gather("vector", *turned[1])
+        out1_tiles("scalar", SHIFT, 4, 4)
+        weave_de(LAST)
+        quant_de_seq(1, SCALE)
+        gate_out0(2, 1, multiply_out0(2, 1, "sum_scale"))
+        quant_de_feat(LAST)
+        store_out0(2)
+        out1_tiles("scalar", SCALE, 0, 4)
+        gate_out0(3, 0, multiply_out0(3, 0, "sum_shift"))
+        out1_tiles("vector", SCALE, 4, 2)
+        gate_out0(3, 1, multiply_out0(3, 1, "sum_scale"))
+        out1_tiles("scalar", SCALE, 6, 2)
+        store_out0(3)

@@ -499,11 +499,9 @@ def tile_temporalcrossattention_pa_v_kernel(
             finish_prod(k, 0)
             gate_da(k, 3)
             normalise(k, 2)
-            if k == 0:
-                normalise(k, 3, nc.vector)
-            else:
-                normalise(k, 3)
+            if k > 0:
                 de_scale(k - 1)
+            normalise(k, 3, nc.vector)
             if has_out0:
                 out0 = [multiply_out0(0, 0, "sum_scale"), multiply_out0(0, 1, "sum_shift")]
             filled = fill_banks(batch2)

from contextlib import ExitStack

import concourse.mybir as mybir
from concourse.masks import make_identity

B, T, D = 512, 4, 1024
FLOPS = 2 * B * T * D * D + 2 * (2 * B * 2 * D * D)
BYTES = 2 * B * T * D * 2 + B * T * D * 4 + B * D * 2 + 3 * D * D * 2 + 2 * D * 2 + 2 * B * T * 4 + B * D * 4 + 2 * D * D * 4

F32 = mybir.dt.float32
BF16 = mybir.dt.bfloat16
U32 = mybir.dt.uint32
U8 = mybir.dt.uint8
E4 = mybir.dt.float8_e4m3fn_x4
E5 = mybir.dt.float8_e5m2_x4
ACT = mybir.ActivationFunctionType
ALU = mybir.AluOpType

P = 128
N = 512
UNITS = 8
LAST = UNITS - 1
SCALE, SHIFT = 0, 1

BANKS = {"da": 3, "sum_shift": 1, "sum_scale": 1, "side": 3}

BATCHES = ((2, 2, 2), (2, 2, 2), (2, 2, 2), (3, 3, 2), (2, 2, 2), (2, 3, 3), (3, 2, 3))


def tile_temporalcrossattention_pa_v_kernel(
    tc, x, y, emb0, We, be, ln2_g, ln2_b, Wo, bo, h, mean, rstd, grad_out, out_0, out_1
):
    nc = tc.nc
    with ExitStack() as ctx:
        keep = ctx.enter_context(tc.tile_pool(name="keep", bufs=1))
        work = ctx.enter_context(tc.tile_pool(name="work", bufs=1))
        psum = ctx.enter_context(tc.psum_pool(name="psum", bufs=1))
        ctx.enter_context(tc.manual_schedule())

        def mx_operand(name, width):
            codes = keep.tile([P, width], U32, name=name + "_codes", align_bytes=64)
            scales = keep.tile([P, width], U8, name=name + "_scales", align_bytes=64)
            return codes, scales

        grad_mx = mx_operand("grad", 4096)
        wo_mx = mx_operand("wo", 2048)
        we_mx = mx_operand("we", 4096)
        emb_mx = mx_operand("emb", 1024)
        de_feat_mx = mx_operand("de_feat", 2048)
        de_seq_mx = mx_operand("de_seq", 1024)

        ident = keep.tile([P, P], F32)
        make_identity(nc, ident[:])
        mean_sb = keep.tile([P, 2, 8], F32)
        rstd_sb = keep.tile([P, 2, 8], F32)
        gain_bias_raw = keep.tile([P, 2, 16], BF16)
        gain_bias = keep.tile([P, 2, 8], F32)

        raw, staged, h_sb, y_sb, silu_sb, tanh_sb, neg_mean = {}, {}, {}, {}, {}, {}, {}
        da, dh, prod, sums, gain_sum, de, woven = {}, {}, {}, {}, {}, {}, {}
        emb_rows, emb_silu_sb, emb_tanh_sb, out1_sb = {}, {}, {}, {}

        def sequences(c):
            u, hi = divmod(c, 2)
            return slice(256 * hi + u, 256 * (hi + 1), 2)

        def span(i):
            return slice(N * i, N * (i + 1))

        def raw_tile(key):
            if key not in raw:
                raw[key] = work.tile([P, 4096], BF16, name="raw", tag="raw", bufs=3, align_bytes=64)
            return raw[key]

        def load_grad(c, pair):
            nc.sync.dma_start(
                out=raw_tile(("grad", c))[:, 2048 * pair : 2048 * (pair + 1)],
                in_=grad_out[sequences(c), 2 * pair : 2 * pair + 2, :].rearrange("q f k -> q (f k)"),
            )

        def load_wo(half, v):
            rows = Wo[span(half), :].rearrange("(m t) k -> m (t k)", t=4)
            piece = slice(2048 * v, 2048 * (v + 1))
            nc.sync.dma_start(out=raw_tile(("wo", half))[:, piece], in_=rows[:, piece])

        def load_we(n, part):
            nc.sync.dma_start(
                out=raw_tile(("we", n, part))[:].rearrange("p (a f) -> p a f", a=4),
                in_=We[span(n), D * part : D * (part + 1)].rearrange("(a p) f -> p a f", p=P),
            )

        def load_emb(n):
            raw["emb", n] = work.tile([P, 4, N], BF16, name="out1", tag="out1", bufs=3)
            nc.sync.dma_start(out=raw["emb", n][:], in_=emb0.rearrange("(p j) d -> p j d", j=4)[:, :, span(n)])

        def load_emb_rows(c):
            emb_rows[c] = work.tile([P, D], BF16, name="emb_rows", tag="emb_rows", bufs=2)
            nc.sync.dma_start(out=emb_rows[c][:], in_=emb0[sequences(c), :])

        def load_h(k, pair):
            half, c = divmod(k, 4)
            h_sb[k, pair] = work.tile([P, 2, N], F32, name="h", tag="h", bufs=4)
            nc.sync.dma_start(out=h_sb[k, pair][:], in_=h[sequences(c), 2 * pair : 2 * pair + 2, span(half)])

        def load_y(k):
            half, c = divmod(k, 4)
            y_sb[k] = work.tile([P, T, N], BF16, name="y", tag="y", bufs=2)
            nc.sync.dma_start(out=y_sb[k][:], in_=y[sequences(c), :, span(half)])

        def load_stats():
            nc.sync.dma_start(out=mean_sb[:], in_=mean.rearrange("(hi q u) f -> q hi (u f)", hi=2, u=2))
            nc.sync.dma_start(out=rstd_sb[:], in_=rstd.rearrange("(hi q u) f -> q hi (u f)", hi=2, u=2))

        def load_gain_bias():
            for i, vec in enumerate((ln2_g, ln2_b)):
                nc.sync.dma_start(
                    out=gain_bias_raw[:, i, 0:8].rearrange("m (half t) -> m half t", half=2),
                    in_=vec.rearrange("(half m t) -> m half t", half=2, t=4),
                )

        def bank(use):
            return psum.tile([P, N], F32, name=use, tag=use, bufs=BANKS[use])

        def staging(key):
            if key not in staged:
                staged[key] = work.tile([P, 4 * N], BF16, name="staged", tag="staged", bufs=4, align_bytes=64)
            return staged[key]

        def turn(blocks, use):
            ps = bank(use)
            for i, block in enumerate(blocks):
                nc.tensor.transpose(ps[:, P * i : P * (i + 1)], block, ident[:])
            return ps

        def every_2nd_word(key, starts):
            words = raw[key][:].bitcast(F32)
            return [words[:, w + u : w + 256 : 2] for w in starts for u in (0, 1)]

        def turn_grad(c, f):
            return turn(every_2nd_word(("grad", c), (512 * f, 512 * f + 256)), "side"), ("grad", c, f // 2), f % 2

        def turn_wo(half, g, v):
            starts = (1024 * v + 256 * g, 1024 * v + 512 + 256 * g)
            return turn(every_2nd_word(("wo", half), starts), "side"), ("wo", half, g), v

        def turn_we(n, part, half, side):
            starts = (1024 * side + 256 * half, 1024 * side + 512 + 256 * half)
            return turn(every_2nd_word(("we", n, part), starts), "side"), ("we", n, part, half), side

        def turn_de(half, part, v, use="side"):
            words = de[half][:].rearrange("m part t b -> m (part t b)").bitcast(F32)
            starts = [(4 * part + 2 * v + e) * 256 + P * u for e in (0, 1) for u in (0, 1)]
            return turn([words[:, w : w + P] for w in starts], use), ("de", half, part), v

        def gather(engine, ps, key, side):
            words = staging(key)[:].bitcast(F32)[:, span(side)].rearrange("p (a m u) -> p a m u", a=2, u=2)
            src = ps[:].rearrange("p (a u m) -> p a m u", a=2, u=2)
            if engine == "scalar":
                nc.scalar.copy(out=words, in_=src)
            else:
                nc.vector.tensor_copy(out=words, in_=src)

        def quantise(src, operand, start, width, fmt):
            codes, scales = operand
            nc.vector.quantize_mx(
                out=codes[:, start : start + width].bitcast(fmt), scales=scales[:, start : start + width], in_=src
            )

        def quant_grad(c, pair):
            quantise(staged["grad", c, pair][:], grad_mx, 1024 * c + N * pair, N, E5)

        def quant_wo(half, g):
            quantise(staged["wo", half, g][:], wo_mx, 1024 * half + N * g, N, E4)

        def quant_we(n, part, half):
            quantise(staged["we", n, part, half][:], we_mx, 2048 * part + 1024 * half + N * n, N, E4)

        def quant_de_seq(half, part):
            quantise(staged["de", half, part][:], de_seq_mx, N * part, N, E5)

        def quant_emb(n):
            quantise(staged["emb", n][:], emb_mx, N * n, N, E4)

        def mx_pass(ps, lhs, lhs_at, lhs_fmt, rhs, rhs_at, rhs_fmt, start, stop):
            nc.tensor.matmul_mx(
                out=ps[:],
                lhsT=lhs[0][:, lhs_at : lhs_at + P].bitcast(lhs_fmt),
                lhsT_scale=lhs[1][:, lhs_at : lhs_at + P],
                rhs=rhs[0][:, rhs_at : rhs_at + N].bitcast(rhs_fmt),
                rhs_scale=rhs[1][:, rhs_at : rhs_at + N],
                start=start,
                stop=stop,
            )

        def multiply_da(k, f):
            half, c = divmod(k, 4)
            da[k, f] = bank("da")
            for g in (0, 1):
                mx_pass(da[k, f], grad_mx, 1024 * c + 256 * f + P * g, E5, wo_mx, 1024 * half + N * g, E4, g == 0, g == 1)

        def activate_h(k, pair, into, name, func, scale):
            into[k, pair] = work.tile([P, 2 * N], F32, name=name, tag=name, bufs=3)
            nc.scalar.activation(
                out=into[k, pair][:].rearrange("q (f e j) -> q f e j", f=2, e=2),
                in_=h_sb[k, pair][:].rearrange("q f (j e) -> q f e j", e=2),
                func=func,
                scale=scale,
            )

        def silu_h(k, pair):
            activate_h(k, pair, silu_sb, "silu", ACT.Silu, -1.0)

        def tanh_h(k, pair):
            activate_h(k, pair, tanh_sb, "tanh", ACT.Tanh, 0.5)

        def gate_da(k, f):
            if f % 2 == 0:
                dh[k, f // 2] = work.tile([P, 2, 2, 256], F32, name="dh", tag="dh", bufs=4)
            nc.vector.scalar_tensor_tensor(
                out=dh[k, f // 2][:, :, f % 2, :],
                in0=tanh_sb[k, f // 2][:, span(f % 2)].rearrange("q (r v) -> q v r", v=2),
                scalar=1.0,
                in1=da[k, f][:].rearrange("q (v r) -> q v r", v=2),
                op0=ALU.add,
                op1=ALU.mult,
            )

        def finish_dh(k, pair):
            both = dh[k, pair][:].rearrange("q v f r -> q v (f r)")
            silu = silu_sb[k, pair][:].rearrange("q (r v) -> q v r", v=2)
            nc.vector.scalar_tensor_tensor(out=both, in0=silu, scalar=1.0, in1=both, op0=ALU.subtract, op1=ALU.mult)

        def negate_mean(k, pair):
            u, hi = divmod(k % 4, 2)
            j = 4 * u + 2 * pair
            neg_mean[k, pair] = work.tile([P, 2], F32, name="neg_mean", tag="neg_mean", bufs=4)
            nc.vector.tensor_scalar(
                out=neg_mean[k, pair][:], in0=mean_sb[:, hi, j : j + 2], scalar1=-1.0, scalar2=None, op0=ALU.mult
            )

        def normalise(k, f, engine=nc.gpsimd):
            u, hi = divmod(k % 4, 2)
            if f % 2 == 0:
                prod[k, f // 2] = work.tile([P, 2, 2, 256], F32, name="prod", tag="prod", bufs=3)
            engine.tensor_scalar(
                out=prod[k, f // 2][:, :, f % 2, :].rearrange("q v (e m) -> q v e m", e=2),
                in0=y_sb[k][:, f, :].rearrange("q (m v e) -> q v e m", v=2, e=2),
                scalar1=neg_mean[k, f // 2][:, f % 2 : f % 2 + 1],
                scalar2=rstd_sb[:, hi, 4 * u + f : 4 * u + f + 1],
                op0=ALU.add,
                op1=ALU.mult,
            )

        def finish_prod(k, pair):
            both = prod[k, pair][:]
            nc.vector.tensor_tensor(out=both, in0=both, in1=dh[k, pair][:], op=ALU.mult)

        def sum_frames(k, part):
            src = prod if part == SCALE else dh
            sums[k, part] = bank("sum_scale" if part == SCALE else "sum_shift")
            for t in range(4):
                for f in range(T):
                    nc.tensor.matmul(
                        sums[k, part][:, P * t : P * (t + 1)],
                        lhsT=src[k, f // 2][:, t // 2, f % 2, P * (t % 2) : P * (t % 2 + 1)],
                        rhs=ident[:],
                        start=(f == 0),
                        stop=(f == T - 1),
                        is_transpose=True,
                    )

        def de_shift(k):
            half, c = divmod(k, 4)
            if c == 0:
                de[half] = work.tile([P, 2, 4, B], BF16, name="de", tag="de", bufs=2, align_bytes=64)
            nc.scalar.activation(
                out=de[half][:, SHIFT, :, P * c : P * (c + 1)],
                in_=sums[k, SHIFT][:].rearrange("m (t q) -> m t q", t=4),
                func=ACT.Copy,
                scale=0.25,
            )

        def apply_gain(k):
            gain_sum[k] = work.tile([P, N], F32, name="gain_sum", tag="gain_sum", bufs=1)
            for t in range(4):
                j = 4 * (k // 4) + t
                nc.scalar.activation(
                    out=gain_sum[k][:, P * t : P * (t + 1)],
                    in_=sums[k, SCALE][:, P * t : P * (t + 1)],
                    func=ACT.Copy,
                    scale=gain_bias[:, 0, j : j + 1],
                )

        def de_scale(k):
            half, c = divmod(k, 4)
            for t in range(4):
                j = 4 * half + t
                nc.vector.scalar_tensor_tensor(
                    out=de[half][:, SCALE, t, P * c : P * (c + 1)],
                    in0=sums[k, SHIFT][:, P * t : P * (t + 1)],
                    scalar=gain_bias[:, 1, j : j + 1],
                    in1=gain_sum[k][:, P * t : P * (t + 1)],
                    op0=ALU.mult,
                    op1=ALU.add,
                )

        def weave_de(k):
            half, c = divmod(k, 4)
            woven[k] = work.tile([P, 2, P, 4], BF16, name="woven", tag="woven", bufs=2, align_bytes=64)
            nc.vector.tensor_copy(
                out=woven[k][:].rearrange("m part (r i) t -> m part r t i", i=4),
                in_=de[half][:, :, :, P * c : P * (c + 1)].rearrange("m part t (r i) -> m part r t i", i=4),
            )

        def quant_de_feat(k):
            quantise(woven[k][:].rearrange("m part q t -> m (part q t)"), de_feat_mx, 256 * k, 256, E5)

        def silu_emb(n):
            nc.scalar.activation(
                out=staging(("emb", n))[:].rearrange("p (d u e) -> p d u e", u=2, e=2),
                in_=raw["emb", n][:].rearrange("p (e u) d -> p d u e", e=2),
                func=ACT.Silu,
            )

        def emb_tanh(c):
            name, depth = ("emb_tanh", 1) if c == 0 else ("tanh", 3)
            emb_tanh_sb[c] = work.tile([P, D], F32, name=name, tag=name, bufs=depth)
            nc.scalar.activation(out=emb_tanh_sb[c][:], in_=emb_rows[c][:], func=ACT.Tanh, scale=0.5)

        def emb_silu(c):
            name, depth = ("emb_silu", 2) if c < 2 else ("silu", 3)
            emb_silu_sb[c] = work.tile([P, D], F32, name=name, tag=name, bufs=depth)
            nc.scalar.activation(out=emb_silu_sb[c][:], in_=emb_rows[c][:], func=ACT.Silu, scale=-1.0)

        def multiply_out0(c, n, use):
            ps = bank(use)
            passes = [(half, part) for half in (0, 1) for part in (SHIFT, SCALE)]
            for i, (half, part) in enumerate(passes):
                de_at = 256 * (4 * half + c) + P * part
                mx_pass(ps, de_feat_mx, de_at, E5, we_mx, 2048 * part + 1024 * half + N * n, E4, i == 0, i == 3)
            return ps

        def gate_out0(c, n, ps):
            cols = emb_tanh_sb[c][:, span(n)]
            nc.vector.scalar_tensor_tensor(out=cols, in0=cols, scalar=1.0, in1=ps[:], op0=ALU.add, op1=ALU.mult)

        def store_out0(c):
            rows = emb_silu_sb[c][:]
            nc.vector.scalar_tensor_tensor(
                out=rows, in0=rows, scalar=1.0, in1=emb_tanh_sb[c][:], op0=ALU.subtract, op1=ALU.mult
            )
            nc.sync.dma_start(out=out_0[sequences(c), :], in_=rows)

        def multiply_out1(part, i, use):
            ps = bank(use)
            mx_pass(ps, emb_mx, P * i, E4, de_seq_mx, N * part, E5, True, True)
            return ps

        def store_out1(engine, half, part, i, ps):
            key = (half, part, i // 2)
            if i % 2 == 0:
                name, depth = ("h", 4) if half == 1 and i % 4 == 0 else ("out1", 3)
                out1_sb[key] = work.tile([P, 2, N], F32, name=name, tag=name, bufs=depth)
            dst = out1_sb[key][:, i % 2, :].rearrange("p (m t) -> p m t", t=4)
            src = ps[:].rearrange("p (t m) -> p m t", t=4)
            if engine == "scalar":
                nc.scalar.activation(out=dst, in_=src, func=ACT.Copy, scale=-2.0)
            else:
                nc.vector.tensor_scalar(out=dst, in0=src, scalar1=-2.0, scalar2=None, op0=ALU.mult)
            if i % 2 == 1:
                f0 = D * part + N * half
                rows = out_1[P * (i - 1) : P * (i + 1), f0 : f0 + N].rearrange("(a p) f -> p a f", p=P)
                nc.sync.dma_start(out=rows, in_=out1_sb[key][:])

        side_jobs = (
            [("grad", c, f) for c in (1, 2, 3) for f in range(T)]
            + [("wo", 1, g, v) for g in (0, 1) for v in (0, 1)]
            + [("we", n, part, half, side) for n in (0, 1) for part in (0, 1) for half in (0, 1) for side in (0, 1)]
            + [("de", 0, part, v) for part in (SHIFT, SCALE) for v in (0, 1)]
            + [("out1", part, i) for part in (SHIFT, SCALE) for i in range(8)]
        )

        def take(count):
            jobs = side_jobs[:count]
            for j in jobs:
                side_jobs.remove(j)
            return jobs

        def fill_banks(jobs):
            turns = {"grad": turn_grad, "wo": turn_wo, "we": turn_we, "de": turn_de}
            return [multiply_out1(*j[1:], "side") if j[0] == "out1" else turns[j[0]](*j[1:]) for j in jobs]

        def empty_banks(jobs, filled, engine="scalar"):
            for j, result in zip(jobs, filled):
                if j[0] == "out1":
                    store_out1(engine, 0, j[1], j[2], result)
                else:
                    gather(engine, *result)

        def quantise_staged(jobs):
            for j in jobs:
                if j[0] == "grad" and j[2] % 2 == 1:
                    quant_grad(j[1], j[2] // 2)
                if j[0] == "wo" and j[3] == 1:
                    quant_wo(j[1], j[2])
                if j[0] == "we" and j[4] == 1:
                    quant_we(j[1], j[2], j[3])
                if j[0] == "de" and j[3] == 1:
                    quant_de_seq(j[1], j[2])

        side_loads = {
            (0, 0): [(load_grad, 3, 0), (load_grad, 3, 1)],
            (0, 1): [(load_wo, 1, 0), (load_wo, 1, 1)],
            (1, 0): [(load_emb, 0), (load_we, 0, 0)],
            (1, 2): [(load_emb, 1), (load_we, 0, 1)],
            (2, 1): [(load_we, 1, 0)],
            (3, 0): [(load_we, 1, 1)],
            (3, 1): [(load_emb_rows, 0), (load_emb_rows, 1)],
            (5, 0): [(load_emb_rows, 2)],
        }

        def load_side(k, point):
            for load in side_loads.get((k, point), []):
                load[0](*load[1:])

        load_wo(0, 0)
        load_wo(0, 1)
        load_grad(0, 0)
        load_grad(0, 1)
        load_h(0, 0)
        load_stats()
        load_h(0, 1)
        load_y(0)
        load_grad(1, 0)
        load_h(1, 0)
        load_grad(1, 1)
        load_h(1, 1)

        for v in (0, 1):
            gather("vector", *turn_wo(0, 0, v))
            gather("scalar", *turn_wo(0, 1, v))
        turned = [turn_grad(0, f) for f in (0, 1)]
        for g in (0, 1):
            quant_wo(0, g)
            gather("scalar", *turned[g])
        turned = [turn_grad(0, f) for f in (2, 3)]
        tanh_h(0, 0)
        gather("vector", *turned[0])
        quant_grad(0, 0)
        gather("vector", *turned[1])
        load_grad(2, 0)
        load_y(1)
        load_grad(2, 1)
        load_gain_bias()
        multiply_da(0, 0)
        multiply_da(0, 1)
        silu_h(0, 0)
        tanh_h(0, 1)
        silu_h(0, 1)
        quant_grad(0, 1)
        multiply_da(0, 2)
        waiting = take(2)
        filled = fill_banks(waiting)
        negate_mean(0, 0)

        for k in range(LAST):
            batch1, batch2, batch3 = [take(count) for count in BATCHES[k]]
            has_out0 = k == LAST - 1
            if k + 2 < UNITS:
                load_h(k + 2, 0)
            load_side(k, 0)
            gate_da(k, 0)
            normalise(k, 0)
            normalise(k, 1)
            if k > 0:
                sum_frames(k - 1, SCALE)
            gate_da(k, 1)
            gate_da(k, 2)
            multiply_da(k, 3)
            silu_h(k + 1, 0)
            tanh_h(k + 1, 0)
            if k == 0:
                empty_banks(waiting, filled, "vector")
            else:
                de_shift(k - 1)
                apply_gain(k - 1)
            finish_dh(k, 0)
            filled = fill_banks(batch1)
            silu_h(k + 1, 1)
            empty_banks(batch1, filled)
            if k + 2 < UNITS:
                load_h(k + 2, 1)
            quantise_staged(waiting)
            multiply_da(k + 1, 0)
            if k in (2, 3):
                quant_emb(k - 2)
            load_side(k, 1)
            negate_mean(k, 1)
            finish_prod(k, 0)
            gate_da(k, 3)
            normalise(k, 2)
            if k > 0:
                de_scale(k - 1)
            normalise(k, 3, nc.vector)
            if has_out0:
                out0 = [multiply_out0(0, 0, "sum_scale"), multiply_out0(0, 1, "sum_shift")]
            filled = fill_banks(batch2)
            if has_out0:
                gate_out0(0, 0, out0[0])
            if k > 0:
                weave_de(k - 1)
            if has_out0:
                gate_out0(0, 1, out0[1])
            quantise_staged(batch1)
            multiply_da(k + 1, 1)
            tanh_h(k + 1, 1)
            empty_banks(batch2, filled)
            load_side(k, 2)
            if k + 2 < UNITS:
                load_y(k + 2)
            if k == 0:
                nc.vector.tensor_scalar(
                    out=gain_bias[:], in0=gain_bias_raw[:, :, 0:8], scalar1=0.25, scalar2=None, op0=ALU.mult
                )
            empty_banks(batch3, fill_banks(batch3))
            multiply_da(k + 1, 2)
            if k in (1, 2):
                silu_emb(k - 1)
            if k == 4:
                emb_tanh(0)
                emb_silu(0)
            finish_dh(k, 1)
            if k > 0:
                quant_de_feat(k - 1)
            quantise_staged(batch2)
            if has_out0:
                store_out0(0)
            sum_frames(k, SHIFT)
            negate_mean(k + 1, 0)
            finish_prod(k, 1)
            if has_out0:
                emb_tanh(1)
                emb_silu(1)
            waiting = batch3

        load_emb_rows(3)
        gate_da(LAST, 0)
        normalise(LAST, 0)
        normalise(LAST, 1)
        sum_frames(LAST - 1, SCALE)
        gate_da(LAST, 1)
        multiply_da(LAST, 3)
        de_shift(LAST - 1)
        apply_gain(LAST - 1)
        empty_banks(side_jobs, fill_banks(side_jobs))
        gate_da(LAST, 2)
        negate_mean(LAST, 1)
        finish_dh(LAST, 0)
        out0 = [multiply_out0(1, n, "da") for n in (0, 1)]
        emb_tanh(2)
        emb_silu(2)
        gate_da(LAST, 3)
        normalise(LAST, 2)
        normalise(LAST, 3)
        de_scale(LAST - 1)
        gate_out0(1, 0, out0[0])
        finish_dh(LAST, 1)
        sum_frames(LAST, SHIFT)
        finish_prod(LAST, 0)
        finish_prod(LAST, 1)
        de_shift(LAST)
        turned = [turn_de(1, SHIFT, v) for v in (0, 1)]
        sum_frames(LAST, SCALE)
        weave_de(LAST - 1)
        gate_out0(1, 1, out0[1])
        emb_tanh(3)
        gather("scalar", *turned[0])
        gather("vector", *turned[1])
        quant_de_feat(LAST - 1)
        quant_de_seq(1, SHIFT)
        emb_silu(3)
        apply_gain(LAST)
        store_out0(1)
        de_scale(LAST)

        def out1_tiles(engine, part, first, count):
            for i in range(first, first + count):
                store_out1(engine, 1, part, i, multiply_out1(part, i, ("side", "da")[i % 2]))

        out1_tiles("scalar", SHIFT, 0, 4)
        ps = multiply_out0(2, 0, "sum_scale")
        turned = [turn_de(1, SCALE, 0, "sum_shift"), turn_de(1, SCALE, 1, "da")]
        gate_out0(2, 0, ps)
        gather("vector", *turned[0])
        gather("vector", *turned[1])
        out1_tiles("scalar", SHIFT, 4, 4)
        weave_de(LAST)
        quant_de_seq(1, SCALE)
        gate_out0(2, 1, multiply_out0(2, 1, "sum_scale"))
        quant_de_feat(LAST)
        store_out0(2)
        out1_tiles("scalar", SCALE, 0, 4)
        gate_out0(3, 0, multiply_out0(3, 0, "sum_shift"))
        out1_tiles("vector", SCALE, 4, 2)
        gate_out0(3, 1, multiply_out0(3, 1, "sum_scale"))
        out1_tiles("scalar", SCALE, 6, 2)
        store_out0(3)
